import numpy as np
import ml_dtypes


def mxq(x, axis, fmt="e4m3"):
    dtype, down = {"e4m3": (ml_dtypes.float8_e4m3fn, 7), "e5m2": (ml_dtypes.float8_e5m2, 14)}[fmt]
    v = np.moveaxis(np.asarray(x, np.float32).astype(ml_dtypes.bfloat16).astype(np.float64), axis, -1)
    blocks = v.reshape(v.shape[:-1] + (-1, 32))
    amax = np.abs(blocks).max(-1, keepdims=True)
    byte = np.maximum(np.where(amax > 0, np.frexp(amax)[1] - 1 + 127, 0) - down, 1)
    scale = np.exp2(byte - 127.0)
    codes = (blocks / scale).astype(np.float32).astype(dtype).astype(np.float64)
    return np.moveaxis((codes * scale).reshape(v.shape), -1, axis)


WIDE = False


def mx_kscale(k):
    if not WIDE:
        return np.ones(k)
    levels = np.array([10, -10, 5, -5, 0])
    a = np.random.permutation(np.resize(levels, k // 512 * 4)).reshape(k // 512, 4)
    idx = np.arange(k)
    return np.exp2(a[idx // 512, idx % 128 // 32])


BF16 = ml_dtypes.bfloat16


def bf(x):
    return np.asarray(x, np.float32).astype(BF16)


def f64(x):
    return np.asarray(x).astype(np.float64)


B, K, N = 2048, 1024, 1024
EPS = 1e-7
MIN_NORM = 1e-15
MAX_TANH_ARG = 15.0


def _cosh(v):
    return 0.5 * (np.exp(v) + np.exp(-v))


def _sinh(v):
    return 0.5 * (np.exp(v) - np.exp(-v))


def _arccosh(v):
    return np.log(v + np.sqrt(v * v - 1.0))


def _norm(v):
    return np.sqrt(np.sum(v * v, axis=-1, keepdims=True))


def _mink_dot(u, v):
    return -u[..., :1] * v[..., :1] + np.sum(u[..., 1:] * v[..., 1:], axis=-1, keepdims=True)


def _proj(x):
    sp = x[..., 1:]
    t = np.sqrt(1.0 + np.sum(sp * sp, axis=-1, keepdims=True))
    return np.concatenate([t, sp], axis=-1)


def _proj_tan(u, x):
    ux = np.sum(x[..., 1:] * u[..., 1:], axis=-1, keepdims=True)
    t = ux / np.maximum(x[..., :1], MIN_NORM)
    return np.concatenate([t, u[..., 1:]], axis=-1)


def logmap_0(x):
    sp = x[..., 1:]
    n = np.maximum(_norm(sp), MIN_NORM)
    theta = np.maximum(x[..., :1], 1.0 + EPS)
    out_sp = _arccosh(theta) * sp / n
    return np.concatenate([np.zeros_like(theta), out_sp], axis=-1)


def expmap_0(u, backproject=True):
    sp = u[..., 1:]
    n = np.maximum(_norm(sp), MIN_NORM)
    theta = np.minimum(n, MAX_TANH_ARG)
    t = _cosh(theta)
    out_sp = _sinh(theta) * sp / n
    res = np.concatenate([t, out_sp], axis=-1)
    return _proj(res) if backproject else res


def ptransp_0(u, x):
    x0 = x[..., :1]
    y = x[..., 1:]
    y_norm = np.maximum(_norm(y), MIN_NORM)
    y_hat = y / y_norm
    v_time = -y_norm
    v_space = (1.0 - x0) * y_hat
    alpha = np.sum(y_hat * u[..., 1:], axis=-1, keepdims=True)
    res_time = np.zeros_like(x0) - alpha * v_time
    res_space = u[..., 1:] - alpha * v_space
    res = np.concatenate([res_time, res_space], axis=-1)
    return _proj_tan(res, x)


def expmap(u, x, backproject=True):
    unorm = np.sqrt(np.maximum(_mink_dot(u, u), MIN_NORM))
    theta = np.minimum(np.maximum(unorm, MIN_NORM), MAX_TANH_ARG)
    res = _cosh(theta) * x + _sinh(theta) * u / theta
    return _proj(res) if backproject else res


def setup_inputs():
    s = mx_kscale(K)
    c = np.sqrt(np.mean(s * s))
    sp = (np.random.standard_normal((B, K)) + 1.0) * (4.0 / np.sqrt(2.0 * K)) * (0.5 + np.random.random((B, 1)))
    sp = sp * s[None, :] / c
    t = np.sqrt(1.0 + np.sum(sp * sp, axis=-1, keepdims=True))
    w0 = np.random.standard_normal((N, K)) * (0.8 / np.sqrt(N))
    p = w0.sum(axis=1)
    b = 0.5 * np.random.standard_normal((1, N)) / np.sqrt(N) + 0.5 * p[None, :] / np.sqrt(np.sum(p * p))
    return {"x": bf(np.concatenate([t, sp], axis=-1)), "weight": bf(w0 / s[None, :] * c), "bias": bf(b)}


def reference(x, weight, bias):
    x, weight, bias = f64(x), f64(weight), f64(bias)
    u = logmap_0(x)
    h_sp = mxq(u[..., 1:], 1, "e4m3") @ mxq(weight, 1, "e4m3").T
    h = np.concatenate([np.zeros_like(h_sp[..., :1]), h_sp], axis=-1)
    m = expmap_0(h, backproject=True)
    b = np.concatenate([np.zeros_like(bias[..., :1]), bias], axis=-1)
    b = np.broadcast_to(b, m.shape)
    pt_b = ptransp_0(b, m)
    return expmap(pt_b, m, backproject=True)

@@ -1,0 +1,388 @@
+from contextlib import ExitStack
+
+import concourse.mybir as mybir
+from concourse.masks import make_identity
+
+FP8X4 = mybir.dt.float8_e4m3fn_x4
+BF16 = mybir.dt.bfloat16
+F32 = mybir.dt.float32
+U32 = mybir.dt.uint32
+U8 = mybir.dt.uint8
+ALU = mybir.AluOpType
+ACT = mybir.ActivationFunctionType
+
+P = 128
+ROWS = 2048
+K = 1024
+N = 1024
+TILES = ROWS // P
+K_PASS = 512
+PASSES = K // K_PASS
+BANK = 512
+BANKS = N // BANK
+W_BLOCKS = N // P
+GROUP = 2
+X_SLOT = 1040
+AHEAD_NORM = 4
+AHEAD_LOG_MAP = 3
+AHEAD_REGROUP = 2
+AHEAD_MATMUL = 1
+
+FLOPS = 2 * ROWS * K * N
+
+
+def tile_hyperboliclinearhyperboloid_kernel(tc, x, weight, bias, out):
+    nc = tc.nc
+    with ExitStack() as stack:
+        keep = stack.enter_context(tc.tile_pool(name="keep", bufs=1))
+        wstage = stack.enter_context(tc.tile_pool(name="wstage", bufs=2))
+        upool = stack.enter_context(tc.tile_pool(name="upool", bufs=4))
+        junk = stack.enter_context(tc.tile_pool(name="junk", bufs=3))
+        small = stack.enter_context(tc.tile_pool(name="small", bufs=8))
+        grp = stack.enter_context(tc.tile_pool(name="grp", bufs=4))
+        psum_t = stack.enter_context(tc.psum_pool(name="psum_t", bufs=2))
+        psum_h = stack.enter_context(tc.psum_pool(name="psum_h", bufs=6))
+        stack.enter_context(tc.manual_schedule())
+
+        x_rows = x.rearrange("(p t) c -> p t c", t=TILES)
+        out_rows = out.rearrange("(p t) c -> p t c", t=TILES)
+        w_rows = weight.rearrange("(b p) k -> p b k", p=P)
+
+        x_head = keep.tile([P, TILES, 16], BF16)
+        nc.sync.dma_start(out=x_head[:], in_=x_rows[:, :, 0:16])
+        bias_bc = keep.tile([P, N], BF16)
+
+        x_sb = keep.tile([P, TILES, X_SLOT], BF16)
+        w_sb = keep.tile([P, W_BLOCKS, K], BF16)
+
+        def load_x(t0, t1):
+            nc.sync.dma_start(out=x_sb[:, t0:t1, 1 : K + 2], in_=x_rows[:, t0:t1, :])
+
+        def load_w(b0, b1):
+            nc.sync.dma_start(out=w_sb[:, b0:b1, :], in_=w_rows[:, b0:b1, :])
+
+        load_x(0, 2)
+        nc.sync.dma_start(out=bias_bc[:], in_=bias.rearrange("a b -> (a b)").partition_broadcast(P))
+        load_w(0, 4)
+        load_w(4, 8)
+        load_x(2, 4)
+        load_x(4, 8)
+        load_x(8, 12)
+        load_x(12, 16)
+
+        ident_f = keep.tile([P, P], F32)
+        make_identity(nc, ident_f[:])
+        half = keep.tile([P, TILES], F32)
+        nc.vector.memset(half[:], 0.5)
+        minus_half = keep.tile([P, 1], F32)
+        nc.vector.memset(minus_half[:], -0.5)
+        warm = keep.tile([P, 1], F32)
+        nc.scalar.activation(out=warm[:], in_=half[:, 0:1], func=ACT.Sqrt)
+
+        theta0 = keep.tile([P, TILES], F32)
+        nc.vector.tensor_scalar(out=theta0[:], in0=x_head[:, :, 0], scalar1=1.0 + 1e-7, scalar2=None, op0=ALU.max)
+        theta0_m1 = keep.tile([P, TILES], F32)
+        nc.vector.tensor_scalar(out=theta0_m1[:], in0=theta0[:], scalar1=-1.0, scalar2=None, op0=ALU.add)
+        theta0_sq = keep.tile([P, TILES], F32)
+        nc.vector.scalar_tensor_tensor(
+            out=theta0_sq[:], in0=theta0[:], scalar=1.0, in1=theta0_m1[:], op0=ALU.add, op1=ALU.mult
+        )
+        theta0_rt = keep.tile([P, TILES], F32)
+        theta0_sum = keep.tile([P, TILES], F32)
+        dist = keep.tile([P, TILES], F32)
+
+        nc.scalar.activation(out=theta0_rt[:], in_=theta0_sq[:], func=ACT.Sqrt)
+        nc.vector.tensor_tensor(out=theta0_sum[:], in0=theta0[:], in1=theta0_rt[:], op=ALU.add)
+        nc.scalar.activation(out=dist[:], in_=theta0_sum[:], func=ACT.Ln)
+
+        bb = keep.tile([P, 1], F32)
+        t_g = keep.tile([P, 3], F32)
+        t_b = t_g[:, 2:3]
+        t_e = keep.tile([P, 2], F32)
+        t_v = keep.tile([P, 6], F32)
+        t_inv = t_v[:, 0:1]
+        cosh_half = t_v[:, 1:2]
+        sinc2 = t_v[:, 2:3]
+        sinc_quarter = t_v[:, 3:4]
+        one_plus = t_v[:, 5:6]
+        bias_s = keep.tile([P, N], F32)
+
+        def bias_norm():
+            junk_b = junk.tile([P, N], F32, tag="junk_a")
+            nc.vector.scalar_tensor_tensor(
+                out=junk_b[:], in0=bias_bc[:], scalar=1.0, in1=bias_bc[:], op0=ALU.mult, op1=ALU.mult, accum_out=bb[:]
+            )
+
+        def bias_root():
+            nc.gpsimd.tensor_scalar(out=t_g[:, 0:1], in0=bb[:], scalar1=1e-15, scalar2=None, op0=ALU.max)
+            nc.gpsimd.tensor_tensor(out=t_g[:, 1:2], in0=t_g[:, 0:1], in1=half[:, 0:1], op=ALU.pow)
+            nc.gpsimd.tensor_scalar(out=t_b, in0=t_g[:, 1:2], scalar1=1e-15, scalar2=15.0, op0=ALU.max, op1=ALU.min)
+
+        def bias_factors():
+            nc.scalar.activation(out=t_e[:, 0:1], in_=t_b, func=ACT.Exp)
+            nc.scalar.activation(out=t_e[:, 1:2], in_=t_b, func=ACT.Exp, scale=-1.0)
+            nc.vector.reciprocal(out=t_inv, in_=t_b)
+            nc.vector.tensor_scalar(
+                out=cosh_half, in0=t_e[:, 0:1], scalar1=t_e[:, 1:2], scalar2=0.25, op0=ALU.add, op1=ALU.mult
+            )
+            nc.vector.scalar_tensor_tensor(
+                out=sinc2, in0=t_e[:, 0:1], scalar=t_e[:, 1:2], in1=t_inv, op0=ALU.subtract, op1=ALU.mult
+            )
+            nc.vector.tensor_scalar(out=sinc_quarter, in0=sinc2, scalar1=0.25, scalar2=None, op0=ALU.mult)
+            nc.vector.scalar_tensor_tensor(
+                out=t_v[:, 4:5], in0=sinc2, scalar=sinc2, in1=bb[:], op0=ALU.mult, op1=ALU.mult
+            )
+            nc.vector.tensor_scalar(out=one_plus, in0=t_v[:, 4:5], scalar1=0.25, scalar2=1.0, op0=ALU.mult, op1=ALU.add)
+
+        def bias_scaled():
+            nc.vector.tensor_scalar(
+                out=bias_s[:], in0=bias_bc[:], scalar1=sinc2, scalar2=0.5, op0=ALU.mult, op1=ALU.mult
+            )
+
+        w_codes = keep.tile([P, PASSES, N], U32, align_bytes=64)
+        w_scales = keep.tile([P, PASSES, N], U8, align_bytes=64)
+        w_words = w_sb[:].bitcast(F32)
+        tiles = {}
+
+        def w_transposes(nh, g):
+            for part in range(2):
+                wt = psum_h.tile([P, BANK], F32, tag="h", name="wt")
+                wt_planes = wt[:].rearrange("p (u n) -> p u n", u=2)
+                for u in range(2):
+                    for b in range(2):
+                        nc.tensor.transpose(
+                            wt_planes[:, u, b * P : (b + 1) * P],
+                            w_words[:, 4 * nh + 2 * part + b, 256 * g + P * u : 256 * g + P * (u + 1)],
+                            ident_f[:],
+                        )
+                tiles[("wt", nh, g, part)] = wt_planes
+
+        def w_quantise(nh, g):
+            w_grouped = wstage.tile([P, BANK, 4], BF16, align_bytes=64, name="w_grouped")
+            w_grouped_words = w_grouped[:].bitcast(F32)
+            for part in range(2):
+                dst = w_grouped_words[:, 2 * P * part : 2 * P * (part + 1), :]
+                src = tiles[("wt", nh, g, part)].rearrange("p u n -> p n u")
+                if part == 0:
+                    nc.vector.tensor_copy(out=dst, in_=src)
+                else:
+                    nc.scalar.copy(out=dst, in_=src)
+            n_cols = slice(nh * BANK, (nh + 1) * BANK)
+            nc.vector.quantize_mx(
+                out=w_codes[:, g, n_cols].bitcast(FP8X4),
+                scales=w_scales[:, g, n_cols],
+                in_=w_grouped[:].rearrange("p n j -> p (n j)"),
+            )
+
+        def sp(t):
+            return x_sb[:, t, 2 : K + 2]
+
+        def group_of(t):
+            key = ("group", t // GROUP)
+            if key not in tiles:
+                tiles[key] = {
+                    "o": grp.tile([P, GROUP, N + 1], F32, name="o_grp"),
+                    "hb": grp.tile([P, GROUP, BANKS], F32, name="hb_grp"),
+                    "hh": grp.tile([P, GROUP], F32, name="hh_grp"),
+                    "a": grp.tile([P, GROUP], F32, name="a_grp"),
+                }
+            return tiles[key], t % GROUP
+
+        def norm_of_sp(t):
+            junk_a = junk.tile([P, K], F32, tag="junk_a", name="junk_a")
+            ss = small.tile([P, 1], F32, name="ss")
+            nc.scalar.activation(out=junk_a[:], in_=sp(t), func=ACT.Square, accum_out=ss[:])
+            rn = small.tile([P, 1], F32, name="rn")
+            nc.gpsimd.tensor_tensor(out=rn[:], in0=ss[:], in1=minus_half[:], op=ALU.pow)
+            tiles[("rn", t)] = rn
+
+        def log_map(t):
+            s_row = small.tile([P, 1], F32, name="s_row")
+            nc.vector.tensor_scalar(
+                out=s_row[:], in0=tiles[("rn", t)][:], scalar1=1e15, scalar2=dist[:, t : t + 1], op0=ALU.min, op1=ALU.mult
+            )
+            u_bf = upool.tile([P, K], BF16, name="u_bf")
+            nc.vector.tensor_scalar(out=u_bf[:], in0=sp(t), scalar1=s_row[:], scalar2=None, op0=ALU.mult)
+            ut = psum_t.tile([P, PASSES, 2, P], F32, tag="tp", name="ut")
+            u_words = u_bf[:].bitcast(F32)
+            for g in range(PASSES):
+                for u in range(2):
+                    nc.tensor.transpose(ut[:, g, u, :], u_words[:, 256 * g + P * u : 256 * g + P * (u + 1)], ident_f[:])
+            tiles[("ut", t)] = ut
+
+        def regroup(t):
+            u_grouped = upool.tile([P, PASSES, P, 4], BF16, align_bytes=64, name="u_grouped")
+            nc.scalar.copy(out=u_grouped[:].bitcast(F32), in_=tiles[("ut", t)][:].rearrange("p g u m -> p g m u"))
+            tiles[("ug", t)] = u_grouped
+
+        def quantise(t):
+            u_codes = upool.tile([P, PASSES * P], U32, align_bytes=64, name="u_codes")
+            u_scales = upool.tile([P, PASSES * P], U8, align_bytes=64, name="u_scales")
+            nc.vector.quantize_mx(
+                out=u_codes[:].bitcast(FP8X4),
+                scales=u_scales[:],
+                in_=tiles[("ug", t)][:].rearrange("p g m j -> p (g m j)"),
+            )
+            tiles[("uq", t)] = (u_codes, u_scales)
+
+        def multiply(t):
+            u_codes, u_scales = tiles[("uq", t)]
+            banks = []
+            for nh in range(BANKS):
+                h = psum_h.tile([P, BANK], F32, tag="h", name="h")
+                for g in range(PASSES):
+                    nc.tensor.matmul_mx(
+                        out=h[:],
+                        lhsT=u_codes[:, g * P : (g + 1) * P].bitcast(FP8X4),
+                        lhsT_scale=u_scales[:, g * P : (g + 1) * P],
+                        rhs=w_codes[:, g, nh * BANK : (nh + 1) * BANK].bitcast(FP8X4),
+                        rhs_scale=w_scales[:, g, nh * BANK : (nh + 1) * BANK],
+                        start=(g == 0),
+                        stop=(g == PASSES - 1),
+                    )
+                banks.append(h)
+            tiles[("h", t)] = banks
+
+        def dot_with_bias(t, nh):
+            group, i = group_of(t)
+            junk_v = junk.tile([P, BANK], F32, name="junk_v")
+            nc.vector.scalar_tensor_tensor(
+                out=junk_v[:], in0=tiles[("h", t)][nh][:], scalar=sinc_quarter,
+                in1=bias_bc[:, nh * BANK : (nh + 1) * BANK],
+                op0=ALU.mult, op1=ALU.mult, accum_out=group["hb"][:, i, nh : nh + 1],
+            )
+
+        def norm_of_h(t):
+            group, i = group_of(t)
+            hh2 = small.tile([P, BANKS], F32, name="hh2")
+            for nh in range(BANKS):
+                junk_s = junk.tile([P, BANK], F32, name="junk_s")
+                nc.scalar.activation(
+                    out=junk_s[:], in_=tiles[("h", t)][nh][:], func=ACT.Square, accum_out=hh2[:, nh : nh + 1]
+                )
+            hh = group["hh"][:, i : i + 1]
+            nc.gpsimd.tensor_scalar(
+                out=hh, in0=hh2[:, 0:1], scalar1=hh2[:, 1:2], scalar2=1e-30, op0=ALU.add, op1=ALU.max
+            )
+            hg = small.tile([P, 2], F32, name="hg")
+            nc.gpsimd.tensor_tensor(out=hg[:, 0:1], in0=hh, in1=minus_half[:], op=ALU.pow)
+            nc.gpsimd.tensor_scalar(
+                out=hg[:, 1:2], in0=hh, scalar1=hg[:, 0:1], scalar2=15.0, op0=ALU.mult, op1=ALU.min
+            )
+            tiles[("hg", t)] = hg
+
+        def exponentials(t):
+            theta = tiles[("hg", t)][:, 1:2]
+            ex = small.tile([P, 3], F32, name="ex")
+            nc.scalar.activation(out=ex[:, 0:1], in_=theta, func=ACT.Exp)
+            nc.scalar.activation(out=ex[:, 1:2], in_=theta, func=ACT.Exp, scale=-1.0)
+            nc.scalar.activation(out=ex[:, 2:3], in_=theta, func=ACT.Tanh, scale=0.5)
+            tiles[("ex", t)] = ex
+
+        def row_factor_parts(t):
+            group, i = group_of(t)
+            ex = tiles[("ex", t)]
+            va = small.tile([P, 3], F32, name="va")
+            nc.vector.scalar_tensor_tensor(
+                out=va[:, 0:1], in0=group["hb"][:, i, 0:1], scalar=group["hb"][:, i, 1:2], in1=ex[:, 2:3],
+                op0=ALU.add, op1=ALU.mult,
+            )
+            nc.vector.scalar_tensor_tensor(
+                out=va[:, 1:2], in0=ex[:, 0:1], scalar=ex[:, 1:2], in1=tiles[("hg", t)][:, 0:1],
+                op0=ALU.subtract, op1=ALU.mult,
+            )
+            tiles[("va", t)] = va
+
+        def row_factor_sum(t):
+            va = tiles[("va", t)]
+            nc.vector.tensor_scalar(
+                out=va[:, 2:3], in0=va[:, 0:1], scalar1=tiles[("hg", t)][:, 0:1], scalar2=cosh_half,
+                op0=ALU.mult, op1=ALU.add,
+            )
+
+        def row_factor(t):
+            group, i = group_of(t)
+            va = tiles[("va", t)]
+            nc.vector.tensor_tensor(out=group["a"][:, i : i + 1], in0=va[:, 2:3], in1=va[:, 1:2], op=ALU.mult)
+
+        def time_coordinate(t):
+            group, i = group_of(t)
+            if i == GROUP - 1:
+                eg = grp.tile([P, 5, GROUP], F32, name="eg")
+                nc.vector.tensor_tensor(out=eg[:, 0, :], in0=group["hb"][:, :, 0], in1=group["hb"][:, :, 1], op=ALU.add)
+                nc.vector.tensor_tensor(out=eg[:, 1, :], in0=group["a"][:], in1=group["hh"][:], op=ALU.mult)
+                nc.vector.scalar_tensor_tensor(
+                    out=eg[:, 2, :], in0=eg[:, 0, :], scalar=4.0, in1=eg[:, 1, :], op0=ALU.mult, op1=ALU.add
+                )
+                nc.vector.tensor_tensor(out=eg[:, 3, :], in0=eg[:, 2, :], in1=group["a"][:], op=ALU.mult)
+                nc.vector.tensor_scalar(out=eg[:, 4, :], in0=eg[:, 3, :], scalar1=one_plus, scalar2=None, op0=ALU.add)
+                time_g = grp.tile([P, GROUP], F32, name="time_g")
+                nc.gpsimd.tensor_tensor(out=time_g[:], in0=eg[:, 4, :], in1=half[:, 0:GROUP], op=ALU.pow)
+                group["time"] = time_g
+
+        def finish(t):
+            group, i = group_of(t)
+            for nh in range(BANKS):
+                nc.vector.scalar_tensor_tensor(
+                    out=group["o"][:, i, 1 + nh * BANK : 1 + (nh + 1) * BANK], in0=tiles[("h", t)][nh][:],
+                    scalar=group["a"][:, i : i + 1], in1=bias_s[:, nh * BANK : (nh + 1) * BANK],
+                    op0=ALU.mult, op1=ALU.add,
+                )
+
+        def store(t):
+            group, i = group_of(t)
+            if i == GROUP - 1:
+                nc.vector.tensor_copy(out=group["o"][:, :, 0], in_=group["time"][:])
+                nc.sync.dma_start(out=out_rows[:, t + 1 - GROUP : t + 1, :], in_=group["o"][:])
+
+        def live(t):
+            return 0 <= t < TILES
+
+        def period(j):
+            if live(j - 2):
+                store(j - 2)
+            if live(j - 1):
+                exponentials(j - 1)
+            if live(j + AHEAD_MATMUL):
+                quantise(j + AHEAD_MATMUL)
+                multiply(j + AHEAD_MATMUL)
+            if live(j - 1):
+                row_factor_parts(j - 1)
+            if live(j):
+                norm_of_h(j)
+                dot_with_bias(j, 0)
+            if live(j - 1):
+                row_factor_sum(j - 1)
+            if live(j):
+                dot_with_bias(j, 1)
+            if live(j - 1):
+                row_factor(j - 1)
+            if live(j + AHEAD_NORM):
+                norm_of_sp(j + AHEAD_NORM)
+            if live(j + AHEAD_LOG_MAP):
+                log_map(j + AHEAD_LOG_MAP)
+            if live(j - 1):
+                time_coordinate(j - 1)
+                finish(j - 1)
+            if live(j + AHEAD_REGROUP):
+                regroup(j + AHEAD_REGROUP)
+
+        def weight_half(nh):
+            for g in range(PASSES):
+                w_transposes(nh, g)
+            for g in range(PASSES):
+                w_quantise(nh, g)
+
+        bias_norm()
+        bias_root()
+        period(-4)
+        weight_half(0)
+        period(-3)
+        bias_factors()
+        weight_half(1)
+        period(-2)
+        period(-1)
+        period(0)
+        bias_scaled()
+        for j in range(1, TILES + 2):
+            period(j)

@@ -39,7 +39,7 @@ def tile_hyperboliclinearhyperboloid_kernel(tc, x, weight, bias, out):
         upool = stack.enter_context(tc.tile_pool(name="upool", bufs=4))
         junk = stack.enter_context(tc.tile_pool(name="junk", bufs=3))
         small = stack.enter_context(tc.tile_pool(name="small", bufs=8))
-        grp = stack.enter_context(tc.tile_pool(name="grp", bufs=4))
+        grp = stack.enter_context(tc.tile_pool(name="grp", bufs=5))
         psum_t = stack.enter_context(tc.psum_pool(name="psum_t", bufs=2))
         psum_h = stack.enter_context(tc.psum_pool(name="psum_h", bufs=6))
         stack.enter_context(tc.manual_schedule())
@@ -157,7 +157,7 @@ def tile_hyperboliclinearhyperboloid_kernel(tc, x, weight, bias, out):
                         )
                 tiles[("wt", nh, g, part)] = wt_planes
 
-        def w_quantise(nh, g):
+        def w_regroup(nh, g):
             w_grouped = wstage.tile([P, BANK, 4], BF16, align_bytes=64, name="w_grouped")
             w_grouped_words = w_grouped[:].bitcast(F32)
             for part in range(2):
@@ -167,11 +167,14 @@ def tile_hyperboliclinearhyperboloid_kernel(tc, x, weight, bias, out):
                     nc.vector.tensor_copy(out=dst, in_=src)
                 else:
                     nc.scalar.copy(out=dst, in_=src)
+            tiles[("wg", nh, g)] = w_grouped
+
+        def w_quantise(nh, g):
             n_cols = slice(nh * BANK, (nh + 1) * BANK)
             nc.vector.quantize_mx(
                 out=w_codes[:, g, n_cols].bitcast(FP8X4),
                 scales=w_scales[:, g, n_cols],
-                in_=w_grouped[:].rearrange("p n j -> p (n j)"),
+                in_=tiles[("wg", nh, g)][:].rearrange("p n j -> p (n j)"),
             )
 
         def sp(t):
@@ -181,10 +184,11 @@ def tile_hyperboliclinearhyperboloid_kernel(tc, x, weight, bias, out):
             key = ("group", t // GROUP)
             if key not in tiles:
                 tiles[key] = {
-                    "o": grp.tile([P, GROUP, N + 1], F32, name="o_grp"),
                     "hb": grp.tile([P, GROUP, BANKS], F32, name="hb_grp"),
+                    "hb4": grp.tile([P, GROUP], F32, name="hb4_grp"),
                     "hh": grp.tile([P, GROUP], F32, name="hh_grp"),
                     "a": grp.tile([P, GROUP], F32, name="a_grp"),
+                    "sq": grp.tile([P, GROUP], F32, name="sq_grp"),
                 }
             return tiles[key], t % GROUP
 
@@ -196,13 +200,16 @@ def tile_hyperboliclinearhyperboloid_kernel(tc, x, weight, bias, out):
             nc.gpsimd.tensor_tensor(out=rn[:], in0=ss[:], in1=minus_half[:], op=ALU.pow)
             tiles[("rn", t)] = rn
 
-        def log_map(t):
+        def row_scale(t):
             s_row = small.tile([P, 1], F32, name="s_row")
             nc.vector.tensor_scalar(
                 out=s_row[:], in0=tiles[("rn", t)][:], scalar1=1e15, scalar2=dist[:, t : t + 1], op0=ALU.min, op1=ALU.mult
             )
+            tiles[("s", t)] = s_row
+
+        def log_map(t):
             u_bf = upool.tile([P, K], BF16, name="u_bf")
-            nc.vector.tensor_scalar(out=u_bf[:], in0=sp(t), scalar1=s_row[:], scalar2=None, op0=ALU.mult)
+            nc.vector.tensor_scalar(out=u_bf[:], in0=sp(t), scalar1=tiles[("s", t)][:], scalar2=None, op0=ALU.mult)
             ut = psum_t.tile([P, PASSES, 2, P], F32, tag="tp", name="ut")
             u_words = u_bf[:].bitcast(F32)
             for g in range(PASSES):
@@ -305,29 +312,42 @@ def tile_hyperboliclinearhyperboloid_kernel(tc, x, weight, bias, out):
             va = tiles[("va", t)]
             nc.vector.tensor_tensor(out=group["a"][:, i : i + 1], in0=va[:, 2:3], in1=va[:, 1:2], op=ALU.mult)
 
-        def time_coordinate(t):
+        def bias_dot_sum(t):
             group, i = group_of(t)
+            nc.vector.tensor_scalar(
+                out=group["hb4"][:, i : i + 1], in0=group["hb"][:, i, 0:1], scalar1=group["hb"][:, i, 1:2], scalar2=4.0,
+                op0=ALU.add, op1=ALU.mult,
+            )
+
+        def time_square_inner(t):
+            group, i = group_of(t)
+            inner = small.tile([P, 1], F32, name="inner")
+            nc.vector.tensor_scalar(
+                out=inner[:], in0=group["hh"][:, i : i + 1], scalar1=group["a"][:, i : i + 1],
+                scalar2=group["hb4"][:, i : i + 1], op0=ALU.mult, op1=ALU.add,
+            )
+            tiles[("inner", t)] = inner
+
+        def time_square(t):
+            group, i = group_of(t)
+            nc.vector.tensor_scalar(
+                out=group["sq"][:, i : i + 1], in0=tiles[("inner", t)][:], scalar1=group["a"][:, i : i + 1],
+                scalar2=one_plus, op0=ALU.mult, op1=ALU.add,
+            )
             if i == GROUP - 1:
-                eg = grp.tile([P, 5, GROUP], F32, name="eg")
-                nc.vector.tensor_tensor(out=eg[:, 0, :], in0=group["hb"][:, :, 0], in1=group["hb"][:, :, 1], op=ALU.add)
-                nc.vector.tensor_tensor(out=eg[:, 1, :], in0=group["a"][:], in1=group["hh"][:], op=ALU.mult)
-                nc.vector.scalar_tensor_tensor(
-                    out=eg[:, 2, :], in0=eg[:, 0, :], scalar=4.0, in1=eg[:, 1, :], op0=ALU.mult, op1=ALU.add
-                )
-                nc.vector.tensor_tensor(out=eg[:, 3, :], in0=eg[:, 2, :], in1=group["a"][:], op=ALU.mult)
-                nc.vector.tensor_scalar(out=eg[:, 4, :], in0=eg[:, 3, :], scalar1=one_plus, scalar2=None, op0=ALU.add)
                 time_g = grp.tile([P, GROUP], F32, name="time_g")
-                nc.gpsimd.tensor_tensor(out=time_g[:], in0=eg[:, 4, :], in1=half[:, 0:GROUP], op=ALU.pow)
+                nc.gpsimd.tensor_tensor(out=time_g[:], in0=group["sq"][:], in1=half[:, 0:GROUP], op=ALU.pow)
                 group["time"] = time_g
 
-        def finish(t):
+        def finish(t, nh):
             group, i = group_of(t)
-            for nh in range(BANKS):
-                nc.vector.scalar_tensor_tensor(
-                    out=group["o"][:, i, 1 + nh * BANK : 1 + (nh + 1) * BANK], in0=tiles[("h", t)][nh][:],
-                    scalar=group["a"][:, i : i + 1], in1=bias_s[:, nh * BANK : (nh + 1) * BANK],
-                    op0=ALU.mult, op1=ALU.add,
-                )
+            if "o" not in group:
+                group["o"] = grp.tile([P, GROUP, N + 1], F32, name="o_grp")
+            nc.vector.scalar_tensor_tensor(
+                out=group["o"][:, i, 1 + nh * BANK : 1 + (nh + 1) * BANK], in0=tiles[("h", t)][nh][:],
+                scalar=group["a"][:, i : i + 1], in1=bias_s[:, nh * BANK : (nh + 1) * BANK],
+                op0=ALU.mult, op1=ALU.add,
+            )
 
         def store(t):
             group, i = group_of(t)
@@ -339,37 +359,48 @@ def tile_hyperboliclinearhyperboloid_kernel(tc, x, weight, bias, out):
             return 0 <= t < TILES
 
         def period(j):
-            if live(j - 2):
-                store(j - 2)
-            if live(j - 1):
-                exponentials(j - 1)
             if live(j + AHEAD_MATMUL):
                 quantise(j + AHEAD_MATMUL)
-                multiply(j + AHEAD_MATMUL)
+            if live(j - 2):
+                finish(j - 2, 0)
+            if live(j + AHEAD_LOG_MAP):
+                row_scale(j + AHEAD_LOG_MAP)
             if live(j - 1):
-                row_factor_parts(j - 1)
+                bias_dot_sum(j - 1)
+            if live(j - 2):
+                finish(j - 2, 1)
+            if live(j + AHEAD_MATMUL):
+                multiply(j + AHEAD_MATMUL)
             if live(j):
                 norm_of_h(j)
                 dot_with_bias(j, 0)
             if live(j - 1):
-                row_factor_sum(j - 1)
+                exponentials(j - 1)
+                row_factor_parts(j - 1)
             if live(j):
                 dot_with_bias(j, 1)
             if live(j - 1):
-                row_factor(j - 1)
+                row_factor_sum(j - 1)
+            if live(j - 2):
+                time_square_inner(j - 2)
             if live(j + AHEAD_NORM):
                 norm_of_sp(j + AHEAD_NORM)
             if live(j + AHEAD_LOG_MAP):
                 log_map(j + AHEAD_LOG_MAP)
             if live(j - 1):
-                time_coordinate(j - 1)
-                finish(j - 1)
+                row_factor(j - 1)
+            if live(j - 2):
+                time_square(j - 2)
             if live(j + AHEAD_REGROUP):
                 regroup(j + AHEAD_REGROUP)
+            if live(j - 3):
+                store(j - 3)
 
         def weight_half(nh):
             for g in range(PASSES):
                 w_transposes(nh, g)
+            for g in range(PASSES):
+                w_regroup(nh, g)
             for g in range(PASSES):
                 w_quantise(nh, g)
 
@@ -384,5 +415,5 @@ def tile_hyperboliclinearhyperboloid_kernel(tc, x, weight, bias, out):
         period(-1)
         period(0)
         bias_scaled()
-        for j in range(1, TILES + 2):
+        for j in range(1, TILES + 3):
             period(j)

@@ -48,9 +48,10 @@ def tile_hyperboliclinearhyperboloid_kernel(tc, x, weight, bias, out):
         out_rows = out.rearrange("(p t) c -> p t c", t=TILES)
         w_rows = weight.rearrange("(b p) k -> p b k", p=P)
 
+        bias_row = keep.tile([P, N], BF16)
+        nc.vector.memset(bias_row[:], 0.0)
+        nc.sync.dma_start(out=bias_row[0:1, :], in_=bias)
         x_head = keep.tile([P, TILES, 16], BF16)
-        nc.sync.dma_start(out=x_head[:], in_=x_rows[:, :, 0:16])
-        bias_bc = keep.tile([P, N], BF16)
 
         x_sb = keep.tile([P, TILES, X_SLOT], BF16)
         w_sb = keep.tile([P, W_BLOCKS, K], BF16)
@@ -62,7 +63,7 @@ def tile_hyperboliclinearhyperboloid_kernel(tc, x, weight, bias, out):
             nc.sync.dma_start(out=w_sb[:, b0:b1, :], in_=w_rows[:, b0:b1, :])
 
         load_x(0, 2)
-        nc.sync.dma_start(out=bias_bc[:], in_=bias.rearrange("a b -> (a b)").partition_broadcast(P))
+        nc.sync.dma_start(out=x_head[:], in_=x_rows[:, :, 0:16])
         load_w(0, 4)
         load_w(4, 8)
         load_x(2, 4)
@@ -72,6 +73,8 @@ def tile_hyperboliclinearhyperboloid_kernel(tc, x, weight, bias, out):
 
         ident_f = keep.tile([P, P], F32)
         make_identity(nc, ident_f[:])
+        ones = keep.tile([P, P], BF16)
+        nc.vector.memset(ones[:], 1.0)
         half = keep.tile([P, TILES], F32)
         nc.vector.memset(half[:], 0.5)
         minus_half = keep.tile([P, 1], F32)
@@ -79,24 +82,27 @@ def tile_hyperboliclinearhyperboloid_kernel(tc, x, weight, bias, out):
         warm = keep.tile([P, 1], F32)
         nc.scalar.activation(out=warm[:], in_=half[:, 0:1], func=ACT.Sqrt)
 
-        theta0 = keep.tile([P, TILES], F32)
-        nc.vector.tensor_scalar(out=theta0[:], in0=x_head[:, :, 0], scalar1=1.0 + 1e-7, scalar2=None, op0=ALU.max)
-        theta0_m1 = keep.tile([P, TILES], F32)
-        nc.vector.tensor_scalar(out=theta0_m1[:], in0=theta0[:], scalar1=-1.0, scalar2=None, op0=ALU.add)
-        theta0_sq = keep.tile([P, TILES], F32)
-        nc.vector.scalar_tensor_tensor(
-            out=theta0_sq[:], in0=theta0[:], scalar=1.0, in1=theta0_m1[:], op0=ALU.add, op1=ALU.mult
-        )
-        theta0_rt = keep.tile([P, TILES], F32)
-        theta0_sum = keep.tile([P, TILES], F32)
         dist = keep.tile([P, TILES], F32)
 
-        nc.scalar.activation(out=theta0_rt[:], in_=theta0_sq[:], func=ACT.Sqrt)
-        nc.vector.tensor_tensor(out=theta0_sum[:], in0=theta0[:], in1=theta0_rt[:], op=ALU.add)
-        nc.scalar.activation(out=dist[:], in_=theta0_sum[:], func=ACT.Ln)
+        def distances():
+            theta0 = keep.tile([P, TILES], F32, name="theta0")
+            nc.vector.tensor_scalar(out=theta0[:], in0=x_head[:, :, 0], scalar1=1.0 + 1e-7, scalar2=None, op0=ALU.max)
+            theta0_m1 = keep.tile([P, TILES], F32, name="theta0_m1")
+            nc.vector.tensor_scalar(out=theta0_m1[:], in0=theta0[:], scalar1=-1.0, scalar2=None, op0=ALU.add)
+            theta0_sq = keep.tile([P, TILES], F32, name="theta0_sq")
+            nc.vector.scalar_tensor_tensor(
+                out=theta0_sq[:], in0=theta0[:], scalar=1.0, in1=theta0_m1[:], op0=ALU.add, op1=ALU.mult
+            )
+            theta0_rt = keep.tile([P, TILES], F32, name="theta0_rt")
+            nc.scalar.activation(out=theta0_rt[:], in_=theta0_sq[:], func=ACT.Sqrt)
+            theta0_sum = keep.tile([P, TILES], F32, name="theta0_sum")
+            nc.vector.tensor_tensor(out=theta0_sum[:], in0=theta0[:], in1=theta0_rt[:], op=ALU.add)
+            nc.scalar.activation(out=dist[:], in_=theta0_sum[:], func=ACT.Ln)
 
-        bb = keep.tile([P, 1], F32)
+        bias_bc = keep.tile([P, N], BF16)
+        bb2 = keep.tile([P, BANKS], F32)
         t_g = keep.tile([P, 3], F32)
+        bb = t_g[:, 0:1]
         t_b = t_g[:, 2:3]
         t_e = keep.tile([P, 2], F32)
         t_v = keep.tile([P, 6], F32)
@@ -107,15 +113,20 @@ def tile_hyperboliclinearhyperboloid_kernel(tc, x, weight, bias, out):
         one_plus = t_v[:, 5:6]
         bias_s = keep.tile([P, N], F32)
 
-        def bias_norm():
-            junk_b = junk.tile([P, N], F32, tag="junk_a")
-            nc.vector.scalar_tensor_tensor(
-                out=junk_b[:], in0=bias_bc[:], scalar=1.0, in1=bias_bc[:], op0=ALU.mult, op1=ALU.mult, accum_out=bb[:]
-            )
+        def bias_spread():
+            for nh in range(BANKS):
+                n_cols = slice(nh * BANK, (nh + 1) * BANK)
+                spread = psum_h.tile([P, BANK], F32, tag="h", name="spread")
+                nc.tensor.matmul(out=spread[:], lhsT=ones[:], rhs=bias_row[:, n_cols], start=True, stop=True)
+                junk_s = junk.tile([P, BANK], F32, name="junk_s")
+                nc.scalar.activation(out=junk_s[:], in_=spread[:], func=ACT.Square, accum_out=bb2[:, nh : nh + 1])
+                nc.vector.tensor_copy(out=bias_bc[:, n_cols], in_=spread[:])
 
         def bias_root():
-            nc.gpsimd.tensor_scalar(out=t_g[:, 0:1], in0=bb[:], scalar1=1e-15, scalar2=None, op0=ALU.max)
-            nc.gpsimd.tensor_tensor(out=t_g[:, 1:2], in0=t_g[:, 0:1], in1=half[:, 0:1], op=ALU.pow)
+            nc.gpsimd.tensor_scalar(
+                out=bb, in0=bb2[:, 0:1], scalar1=bb2[:, 1:2], scalar2=1e-15, op0=ALU.add, op1=ALU.max
+            )
+            nc.gpsimd.tensor_tensor(out=t_g[:, 1:2], in0=bb, in1=half[:, 0:1], op=ALU.pow)
             nc.gpsimd.tensor_scalar(out=t_b, in0=t_g[:, 1:2], scalar1=1e-15, scalar2=15.0, op0=ALU.max, op1=ALU.min)
 
         def bias_factors():
@@ -130,7 +141,7 @@ def tile_hyperboliclinearhyperboloid_kernel(tc, x, weight, bias, out):
             )
             nc.vector.tensor_scalar(out=sinc_quarter, in0=sinc2, scalar1=0.25, scalar2=None, op0=ALU.mult)
             nc.vector.scalar_tensor_tensor(
-                out=t_v[:, 4:5], in0=sinc2, scalar=sinc2, in1=bb[:], op0=ALU.mult, op1=ALU.mult
+                out=t_v[:, 4:5], in0=sinc2, scalar=sinc2, in1=bb, op0=ALU.mult, op1=ALU.mult
             )
             nc.vector.tensor_scalar(out=one_plus, in0=t_v[:, 4:5], scalar1=0.25, scalar2=1.0, op0=ALU.mult, op1=ALU.add)
 
@@ -362,12 +373,14 @@ def tile_hyperboliclinearhyperboloid_kernel(tc, x, weight, bias, out):
             if live(j + AHEAD_MATMUL):
                 quantise(j + AHEAD_MATMUL)
             if live(j - 2):
+                time_square_inner(j - 2)
                 finish(j - 2, 0)
             if live(j + AHEAD_LOG_MAP):
                 row_scale(j + AHEAD_LOG_MAP)
             if live(j - 1):
                 bias_dot_sum(j - 1)
             if live(j - 2):
+                time_square(j - 2)
                 finish(j - 2, 1)
             if live(j + AHEAD_MATMUL):
                 multiply(j + AHEAD_MATMUL)
@@ -381,20 +394,16 @@ def tile_hyperboliclinearhyperboloid_kernel(tc, x, weight, bias, out):
                 dot_with_bias(j, 1)
             if live(j - 1):
                 row_factor_sum(j - 1)
-            if live(j - 2):
-                time_square_inner(j - 2)
             if live(j + AHEAD_NORM):
                 norm_of_sp(j + AHEAD_NORM)
             if live(j + AHEAD_LOG_MAP):
                 log_map(j + AHEAD_LOG_MAP)
             if live(j - 1):
                 row_factor(j - 1)
-            if live(j - 2):
-                time_square(j - 2)
             if live(j + AHEAD_REGROUP):
                 regroup(j + AHEAD_REGROUP)
-            if live(j - 3):
-                store(j - 3)
+            if live(j - 2):
+                store(j - 2)
 
         def weight_half(nh):
             for g in range(PASSES):
@@ -404,16 +413,18 @@ def tile_hyperboliclinearhyperboloid_kernel(tc, x, weight, bias, out):
             for g in range(PASSES):
                 w_quantise(nh, g)
 
-        bias_norm()
+        bias_spread()
         bias_root()
-        period(-4)
+        norm_of_sp(0)
+        norm_of_sp(1)
+        distances()
+        row_scale(0)
+        log_map(0)
         weight_half(0)
-        period(-3)
         bias_factors()
         weight_half(1)
-        period(-2)
-        period(-1)
-        period(0)
+        for j in range(-2, 1):
+            period(j)
         bias_scaled()
-        for j in range(1, TILES + 3):
+        for j in range(1, TILES + 2):
             period(j)

@@ -20,8 +20,8 @@ K_PASS = 512
 PASSES = K // K_PASS
 BANK = 512
 BANKS = N // BANK
-W_BLOCKS = N // P
-GROUP = 2
+W_CHUNK = 256
+W_CHUNKS = N // W_CHUNK
 X_SLOT = 1040
 AHEAD_NORM = 4
 AHEAD_LOG_MAP = 3
@@ -35,74 +35,69 @@ def tile_hyperboliclinearhyperboloid_kernel(tc, x, weight, bias, out):
     nc = tc.nc
     with ExitStack() as stack:
         keep = stack.enter_context(tc.tile_pool(name="keep", bufs=1))
-        wstage = stack.enter_context(tc.tile_pool(name="wstage", bufs=2))
+        wstage = stack.enter_context(tc.tile_pool(name="wstage", bufs=4))
         upool = stack.enter_context(tc.tile_pool(name="upool", bufs=4))
+        opool = stack.enter_context(tc.tile_pool(name="opool", bufs=4))
         junk = stack.enter_context(tc.tile_pool(name="junk", bufs=3))
         small = stack.enter_context(tc.tile_pool(name="small", bufs=8))
-        grp = stack.enter_context(tc.tile_pool(name="grp", bufs=5))
-        psum_t = stack.enter_context(tc.psum_pool(name="psum_t", bufs=2))
-        psum_h = stack.enter_context(tc.psum_pool(name="psum_h", bufs=6))
+        psum_t = stack.enter_context(tc.psum_pool(name="psum_t", bufs=1))
+        psum_h = stack.enter_context(tc.psum_pool(name="psum_h", bufs=7))
         stack.enter_context(tc.manual_schedule())
 
         x_rows = x.rearrange("(p t) c -> p t c", t=TILES)
         out_rows = out.rearrange("(p t) c -> p t c", t=TILES)
-        w_rows = weight.rearrange("(b p) k -> p b k", p=P)
+        w_rows = weight.rearrange("(c b p) k -> p c b k", b=W_CHUNK // P, p=P)
 
-        bias_row = keep.tile([P, N], BF16)
-        nc.vector.memset(bias_row[:], 0.0)
-        nc.sync.dma_start(out=bias_row[0:1, :], in_=bias)
         x_head = keep.tile([P, TILES, 16], BF16)
-
+        bias_bc = keep.tile([P, N], BF16)
         x_sb = keep.tile([P, TILES, X_SLOT], BF16)
-        w_sb = keep.tile([P, W_BLOCKS, K], BF16)
+        w_sb = keep.tile([P, W_CHUNKS, W_CHUNK // P, K], BF16)
 
         def load_x(t0, t1):
             nc.sync.dma_start(out=x_sb[:, t0:t1, 1 : K + 2], in_=x_rows[:, t0:t1, :])
 
-        def load_w(b0, b1):
-            nc.sync.dma_start(out=w_sb[:, b0:b1, :], in_=w_rows[:, b0:b1, :])
+        def load_w(c):
+            nc.sync.dma_start(out=w_sb[:, c, :, :], in_=w_rows[:, c, :, :])
 
-        load_x(0, 2)
         nc.sync.dma_start(out=x_head[:], in_=x_rows[:, :, 0:16])
-        load_w(0, 4)
-        load_w(4, 8)
+        load_x(0, 2)
+        nc.sync.dma_start(out=bias_bc[:], in_=bias.rearrange("a b -> (a b)").partition_broadcast(P))
+        load_w(0)
+        load_w(1)
         load_x(2, 4)
-        load_x(4, 8)
+        load_w(2)
+        load_w(3)
+        load_x(4, 6)
+        load_x(6, 8)
         load_x(8, 12)
         load_x(12, 16)
 
         ident_f = keep.tile([P, P], F32)
         make_identity(nc, ident_f[:])
-        ones = keep.tile([P, P], BF16)
-        nc.vector.memset(ones[:], 1.0)
-        half = keep.tile([P, TILES], F32)
+        half = keep.tile([P, 1], F32)
         nc.vector.memset(half[:], 0.5)
         minus_half = keep.tile([P, 1], F32)
         nc.vector.memset(minus_half[:], -0.5)
         warm = keep.tile([P, 1], F32)
-        nc.scalar.activation(out=warm[:], in_=half[:, 0:1], func=ACT.Sqrt)
+        nc.scalar.activation(out=warm[:], in_=half[:], func=ACT.Sqrt)
 
+        theta0 = keep.tile([P, TILES], F32)
+        nc.vector.tensor_scalar(out=theta0[:], in0=x_head[:, :, 0], scalar1=1.0 + 1e-7, scalar2=None, op0=ALU.max)
+        theta0_m1 = keep.tile([P, TILES], F32)
+        nc.vector.tensor_scalar(out=theta0_m1[:], in0=theta0[:], scalar1=-1.0, scalar2=None, op0=ALU.add)
+        theta0_sq = keep.tile([P, TILES], F32)
+        nc.vector.scalar_tensor_tensor(
+            out=theta0_sq[:], in0=theta0[:], scalar=1.0, in1=theta0_m1[:], op0=ALU.add, op1=ALU.mult
+        )
+        theta0_rt = keep.tile([P, TILES], F32)
+        nc.scalar.activation(out=theta0_rt[:], in_=theta0_sq[:], func=ACT.Sqrt)
+        theta0_sum = keep.tile([P, TILES], F32)
+        nc.vector.tensor_tensor(out=theta0_sum[:], in0=theta0[:], in1=theta0_rt[:], op=ALU.add)
         dist = keep.tile([P, TILES], F32)
+        nc.scalar.activation(out=dist[:], in_=theta0_sum[:], func=ACT.Ln)
 
-        def distances():
-            theta0 = keep.tile([P, TILES], F32, name="theta0")
-            nc.vector.tensor_scalar(out=theta0[:], in0=x_head[:, :, 0], scalar1=1.0 + 1e-7, scalar2=None, op0=ALU.max)
-            theta0_m1 = keep.tile([P, TILES], F32, name="theta0_m1")
-            nc.vector.tensor_scalar(out=theta0_m1[:], in0=theta0[:], scalar1=-1.0, scalar2=None, op0=ALU.add)
-            theta0_sq = keep.tile([P, TILES], F32, name="theta0_sq")
-            nc.vector.scalar_tensor_tensor(
-                out=theta0_sq[:], in0=theta0[:], scalar=1.0, in1=theta0_m1[:], op0=ALU.add, op1=ALU.mult
-            )
-            theta0_rt = keep.tile([P, TILES], F32, name="theta0_rt")
-            nc.scalar.activation(out=theta0_rt[:], in_=theta0_sq[:], func=ACT.Sqrt)
-            theta0_sum = keep.tile([P, TILES], F32, name="theta0_sum")
-            nc.vector.tensor_tensor(out=theta0_sum[:], in0=theta0[:], in1=theta0_rt[:], op=ALU.add)
-            nc.scalar.activation(out=dist[:], in_=theta0_sum[:], func=ACT.Ln)
-
-        bias_bc = keep.tile([P, N], BF16)
-        bb2 = keep.tile([P, BANKS], F32)
+        bb = keep.tile([P, 1], F32)
         t_g = keep.tile([P, 3], F32)
-        bb = t_g[:, 0:1]
         t_b = t_g[:, 2:3]
         t_e = keep.tile([P, 2], F32)
         t_v = keep.tile([P, 6], F32)
@@ -113,20 +108,13 @@ def tile_hyperboliclinearhyperboloid_kernel(tc, x, weight, bias, out):
         one_plus = t_v[:, 5:6]
         bias_s = keep.tile([P, N], F32)
 
-        def bias_spread():
-            for nh in range(BANKS):
-                n_cols = slice(nh * BANK, (nh + 1) * BANK)
-                spread = psum_h.tile([P, BANK], F32, tag="h", name="spread")
-                nc.tensor.matmul(out=spread[:], lhsT=ones[:], rhs=bias_row[:, n_cols], start=True, stop=True)
-                junk_s = junk.tile([P, BANK], F32, name="junk_s")
-                nc.scalar.activation(out=junk_s[:], in_=spread[:], func=ACT.Square, accum_out=bb2[:, nh : nh + 1])
-                nc.vector.tensor_copy(out=bias_bc[:, n_cols], in_=spread[:])
-
-        def bias_root():
-            nc.gpsimd.tensor_scalar(
-                out=bb, in0=bb2[:, 0:1], scalar1=bb2[:, 1:2], scalar2=1e-15, op0=ALU.add, op1=ALU.max
+        def bias_norm():
+            junk_b = junk.tile([P, N], F32, tag="junk_a")
+            nc.vector.scalar_tensor_tensor(
+                out=junk_b[:], in0=bias_bc[:], scalar=1.0, in1=bias_bc[:], op0=ALU.mult, op1=ALU.mult, accum_out=bb[:]
             )
-            nc.gpsimd.tensor_tensor(out=t_g[:, 1:2], in0=bb, in1=half[:, 0:1], op=ALU.pow)
+            nc.gpsimd.tensor_scalar(out=t_g[:, 0:1], in0=bb[:], scalar1=1e-15, scalar2=None, op0=ALU.max)
+            nc.gpsimd.tensor_tensor(out=t_g[:, 1:2], in0=t_g[:, 0:1], in1=half[:], op=ALU.pow)
             nc.gpsimd.tensor_scalar(out=t_b, in0=t_g[:, 1:2], scalar1=1e-15, scalar2=15.0, op0=ALU.max, op1=ALU.min)
 
         def bias_factors():
@@ -141,7 +129,7 @@ def tile_hyperboliclinearhyperboloid_kernel(tc, x, weight, bias, out):
             )
             nc.vector.tensor_scalar(out=sinc_quarter, in0=sinc2, scalar1=0.25, scalar2=None, op0=ALU.mult)
             nc.vector.scalar_tensor_tensor(
-                out=t_v[:, 4:5], in0=sinc2, scalar=sinc2, in1=bb, op0=ALU.mult, op1=ALU.mult
+                out=t_v[:, 4:5], in0=sinc2, scalar=sinc2, in1=bb[:], op0=ALU.mult, op1=ALU.mult
             )
             nc.vector.tensor_scalar(out=one_plus, in0=t_v[:, 4:5], scalar1=0.25, scalar2=1.0, op0=ALU.mult, op1=ALU.add)
 
@@ -153,55 +141,36 @@ def tile_hyperboliclinearhyperboloid_kernel(tc, x, weight, bias, out):
         w_codes = keep.tile([P, PASSES, N], U32, align_bytes=64)
         w_scales = keep.tile([P, PASSES, N], U8, align_bytes=64)
         w_words = w_sb[:].bitcast(F32)
-        tiles = {}
 
-        def w_transposes(nh, g):
-            for part in range(2):
-                wt = psum_h.tile([P, BANK], F32, tag="h", name="wt")
-                wt_planes = wt[:].rearrange("p (u n) -> p u n", u=2)
+        def weight_chunk(c):
+            grouped = []
+            for g in range(PASSES):
+                wt = psum_h.tile([P, 2, W_CHUNK], F32, tag="h", name="wt")
                 for u in range(2):
-                    for b in range(2):
+                    for b in range(W_CHUNK // P):
                         nc.tensor.transpose(
-                            wt_planes[:, u, b * P : (b + 1) * P],
-                            w_words[:, 4 * nh + 2 * part + b, 256 * g + P * u : 256 * g + P * (u + 1)],
+                            wt[:, u, b * P : (b + 1) * P],
+                            w_words[:, c, b, 256 * g + P * u : 256 * g + P * (u + 1)],
                             ident_f[:],
                         )
-                tiles[("wt", nh, g, part)] = wt_planes
-
-        def w_regroup(nh, g):
-            w_grouped = wstage.tile([P, BANK, 4], BF16, align_bytes=64, name="w_grouped")
-            w_grouped_words = w_grouped[:].bitcast(F32)
-            for part in range(2):
-                dst = w_grouped_words[:, 2 * P * part : 2 * P * (part + 1), :]
-                src = tiles[("wt", nh, g, part)].rearrange("p u n -> p n u")
-                if part == 0:
-                    nc.vector.tensor_copy(out=dst, in_=src)
+                w_grouped = wstage.tile([P, W_CHUNK, 4], BF16, align_bytes=64, name="w_grouped")
+                if g == 0:
+                    nc.vector.tensor_copy(out=w_grouped[:].bitcast(F32), in_=wt[:].rearrange("p u n -> p n u"))
                 else:
-                    nc.scalar.copy(out=dst, in_=src)
-            tiles[("wg", nh, g)] = w_grouped
+                    nc.scalar.copy(out=w_grouped[:].bitcast(F32), in_=wt[:].rearrange("p u n -> p n u"))
+                grouped.append(w_grouped)
+            n_cols = slice(c * W_CHUNK, (c + 1) * W_CHUNK)
+            for g in reversed(range(PASSES)):
+                nc.vector.quantize_mx(
+                    out=w_codes[:, g, n_cols].bitcast(FP8X4),
+                    scales=w_scales[:, g, n_cols],
+                    in_=grouped[g][:].rearrange("p n j -> p (n j)"),
+                )
 
-        def w_quantise(nh, g):
-            n_cols = slice(nh * BANK, (nh + 1) * BANK)
-            nc.vector.quantize_mx(
-                out=w_codes[:, g, n_cols].bitcast(FP8X4),
-                scales=w_scales[:, g, n_cols],
-                in_=tiles[("wg", nh, g)][:].rearrange("p n j -> p (n j)"),
-            )
+        tiles = {}
 
         def sp(t):
             return x_sb[:, t, 2 : K + 2]
-
-        def group_of(t):
-            key = ("group", t // GROUP)
-            if key not in tiles:
-                tiles[key] = {
-                    "hb": grp.tile([P, GROUP, BANKS], F32, name="hb_grp"),
-                    "hb4": grp.tile([P, GROUP], F32, name="hb4_grp"),
-                    "hh": grp.tile([P, GROUP], F32, name="hh_grp"),
-                    "a": grp.tile([P, GROUP], F32, name="a_grp"),
-                    "sq": grp.tile([P, GROUP], F32, name="sq_grp"),
-                }
-            return tiles[key], t % GROUP
 
         def norm_of_sp(t):
             junk_a = junk.tile([P, K], F32, tag="junk_a", name="junk_a")
@@ -221,7 +190,7 @@ def tile_hyperboliclinearhyperboloid_kernel(tc, x, weight, bias, out):
         def log_map(t):
             u_bf = upool.tile([P, K], BF16, name="u_bf")
             nc.vector.tensor_scalar(out=u_bf[:], in0=sp(t), scalar1=tiles[("s", t)][:], scalar2=None, op0=ALU.mult)
-            ut = psum_t.tile([P, PASSES, 2, P], F32, tag="tp", name="ut")
+            ut = psum_t.tile([P, PASSES, 2, P], F32, name="ut")
             u_words = u_bf[:].bitcast(F32)
             for g in range(PASSES):
                 for u in range(2):
@@ -243,54 +212,50 @@ def tile_hyperboliclinearhyperboloid_kernel(tc, x, weight, bias, out):
             )
             tiles[("uq", t)] = (u_codes, u_scales)
 
-        def multiply(t):
+        def multiply(t, nh):
             u_codes, u_scales = tiles[("uq", t)]
-            banks = []
-            for nh in range(BANKS):
-                h = psum_h.tile([P, BANK], F32, tag="h", name="h")
-                for g in range(PASSES):
-                    nc.tensor.matmul_mx(
-                        out=h[:],
-                        lhsT=u_codes[:, g * P : (g + 1) * P].bitcast(FP8X4),
-                        lhsT_scale=u_scales[:, g * P : (g + 1) * P],
-                        rhs=w_codes[:, g, nh * BANK : (nh + 1) * BANK].bitcast(FP8X4),
-                        rhs_scale=w_scales[:, g, nh * BANK : (nh + 1) * BANK],
-                        start=(g == 0),
-                        stop=(g == PASSES - 1),
-                    )
-                banks.append(h)
-            tiles[("h", t)] = banks
-
-        def dot_with_bias(t, nh):
-            group, i = group_of(t)
-            junk_v = junk.tile([P, BANK], F32, name="junk_v")
-            nc.vector.scalar_tensor_tensor(
-                out=junk_v[:], in0=tiles[("h", t)][nh][:], scalar=sinc_quarter,
-                in1=bias_bc[:, nh * BANK : (nh + 1) * BANK],
-                op0=ALU.mult, op1=ALU.mult, accum_out=group["hb"][:, i, nh : nh + 1],
-            )
+            h = psum_h.tile([P, BANK], F32, tag="h", name="h")
+            for g in range(PASSES):
+                nc.tensor.matmul_mx(
+                    out=h[:],
+                    lhsT=u_codes[:, g * P : (g + 1) * P].bitcast(FP8X4),
+                    lhsT_scale=u_scales[:, g * P : (g + 1) * P],
+                    rhs=w_codes[:, g, nh * BANK : (nh + 1) * BANK].bitcast(FP8X4),
+                    rhs_scale=w_scales[:, g, nh * BANK : (nh + 1) * BANK],
+                    start=(g == 0),
+                    stop=(g == PASSES - 1),
+                )
+            tiles[("h", t, nh)] = h
 
         def norm_of_h(t):
-            group, i = group_of(t)
             hh2 = small.tile([P, BANKS], F32, name="hh2")
             for nh in range(BANKS):
                 junk_s = junk.tile([P, BANK], F32, name="junk_s")
                 nc.scalar.activation(
-                    out=junk_s[:], in_=tiles[("h", t)][nh][:], func=ACT.Square, accum_out=hh2[:, nh : nh + 1]
+                    out=junk_s[:], in_=tiles[("h", t, nh)][:], func=ACT.Square, accum_out=hh2[:, nh : nh + 1]
                 )
-            hh = group["hh"][:, i : i + 1]
+            hg = small.tile([P, 3], F32, name="hg")
             nc.gpsimd.tensor_scalar(
-                out=hh, in0=hh2[:, 0:1], scalar1=hh2[:, 1:2], scalar2=1e-30, op0=ALU.add, op1=ALU.max
+                out=hg[:, 0:1], in0=hh2[:, 0:1], scalar1=hh2[:, 1:2], scalar2=1e-30, op0=ALU.add, op1=ALU.max
             )
-            hg = small.tile([P, 2], F32, name="hg")
-            nc.gpsimd.tensor_tensor(out=hg[:, 0:1], in0=hh, in1=minus_half[:], op=ALU.pow)
+            nc.gpsimd.tensor_tensor(out=hg[:, 1:2], in0=hg[:, 0:1], in1=minus_half[:], op=ALU.pow)
             nc.gpsimd.tensor_scalar(
-                out=hg[:, 1:2], in0=hh, scalar1=hg[:, 0:1], scalar2=15.0, op0=ALU.mult, op1=ALU.min
+                out=hg[:, 2:3], in0=hg[:, 0:1], scalar1=hg[:, 1:2], scalar2=15.0, op0=ALU.mult, op1=ALU.min
             )
             tiles[("hg", t)] = hg
 
+        def dot_with_bias(t, nh):
+            if nh == 0:
+                tiles[("hb", t)] = small.tile([P, BANKS], F32, name="hb")
+            junk_v = junk.tile([P, BANK], F32, name="junk_v")
+            nc.vector.scalar_tensor_tensor(
+                out=junk_v[:], in0=tiles[("h", t, nh)][:], scalar=sinc_quarter,
+                in1=bias_bc[:, nh * BANK : (nh + 1) * BANK],
+                op0=ALU.mult, op1=ALU.mult, accum_out=tiles[("hb", t)][:, nh : nh + 1],
+            )
+
         def exponentials(t):
-            theta = tiles[("hg", t)][:, 1:2]
+            theta = tiles[("hg", t)][:, 2:3]
             ex = small.tile([P, 3], F32, name="ex")
             nc.scalar.activation(out=ex[:, 0:1], in_=theta, func=ACT.Exp)
             nc.scalar.activation(out=ex[:, 1:2], in_=theta, func=ACT.Exp, scale=-1.0)
@@ -298,92 +263,80 @@ def tile_hyperboliclinearhyperboloid_kernel(tc, x, weight, bias, out):
             tiles[("ex", t)] = ex
 
         def row_factor_parts(t):
-            group, i = group_of(t)
             ex = tiles[("ex", t)]
-            va = small.tile([P, 3], F32, name="va")
+            hb = tiles[("hb", t)]
+            va = small.tile([P, 7], F32, name="va")
             nc.vector.scalar_tensor_tensor(
-                out=va[:, 0:1], in0=group["hb"][:, i, 0:1], scalar=group["hb"][:, i, 1:2], in1=ex[:, 2:3],
-                op0=ALU.add, op1=ALU.mult,
+                out=va[:, 0:1], in0=hb[:, 0:1], scalar=hb[:, 1:2], in1=ex[:, 2:3], op0=ALU.add, op1=ALU.mult
             )
             nc.vector.scalar_tensor_tensor(
-                out=va[:, 1:2], in0=ex[:, 0:1], scalar=ex[:, 1:2], in1=tiles[("hg", t)][:, 0:1],
+                out=va[:, 1:2], in0=ex[:, 0:1], scalar=ex[:, 1:2], in1=tiles[("hg", t)][:, 1:2],
                 op0=ALU.subtract, op1=ALU.mult,
+            )
+            nc.vector.tensor_scalar(
+                out=va[:, 4:5], in0=hb[:, 0:1], scalar1=hb[:, 1:2], scalar2=4.0, op0=ALU.add, op1=ALU.mult
             )
             tiles[("va", t)] = va
 
         def row_factor_sum(t):
             va = tiles[("va", t)]
             nc.vector.tensor_scalar(
-                out=va[:, 2:3], in0=va[:, 0:1], scalar1=tiles[("hg", t)][:, 0:1], scalar2=cosh_half,
+                out=va[:, 2:3], in0=va[:, 0:1], scalar1=tiles[("hg", t)][:, 1:2], scalar2=cosh_half,
                 op0=ALU.mult, op1=ALU.add,
             )
 
         def row_factor(t):
-            group, i = group_of(t)
             va = tiles[("va", t)]
-            nc.vector.tensor_tensor(out=group["a"][:, i : i + 1], in0=va[:, 2:3], in1=va[:, 1:2], op=ALU.mult)
-
-        def bias_dot_sum(t):
-            group, i = group_of(t)
-            nc.vector.tensor_scalar(
-                out=group["hb4"][:, i : i + 1], in0=group["hb"][:, i, 0:1], scalar1=group["hb"][:, i, 1:2], scalar2=4.0,
-                op0=ALU.add, op1=ALU.mult,
-            )
+            nc.vector.tensor_tensor(out=va[:, 3:4], in0=va[:, 2:3], in1=va[:, 1:2], op=ALU.mult)
 
         def time_square_inner(t):
-            group, i = group_of(t)
-            inner = small.tile([P, 1], F32, name="inner")
+            va = tiles[("va", t)]
             nc.vector.tensor_scalar(
-                out=inner[:], in0=group["hh"][:, i : i + 1], scalar1=group["a"][:, i : i + 1],
-                scalar2=group["hb4"][:, i : i + 1], op0=ALU.mult, op1=ALU.add,
+                out=va[:, 5:6], in0=tiles[("hg", t)][:, 0:1], scalar1=va[:, 3:4], scalar2=va[:, 4:5],
+                op0=ALU.mult, op1=ALU.add,
             )
-            tiles[("inner", t)] = inner
 
         def time_square(t):
-            group, i = group_of(t)
+            va = tiles[("va", t)]
             nc.vector.tensor_scalar(
-                out=group["sq"][:, i : i + 1], in0=tiles[("inner", t)][:], scalar1=group["a"][:, i : i + 1],
-                scalar2=one_plus, op0=ALU.mult, op1=ALU.add,
+                out=va[:, 6:7], in0=va[:, 5:6], scalar1=va[:, 3:4], scalar2=one_plus, op0=ALU.mult, op1=ALU.add
             )
-            if i == GROUP - 1:
-                time_g = grp.tile([P, GROUP], F32, name="time_g")
-                nc.gpsimd.tensor_tensor(out=time_g[:], in0=group["sq"][:], in1=half[:, 0:GROUP], op=ALU.pow)
-                group["time"] = time_g
+            time_g = small.tile([P, 1], F32, name="time_g")
+            nc.gpsimd.tensor_tensor(out=time_g[:], in0=va[:, 6:7], in1=half[:], op=ALU.pow)
+            tiles[("time", t)] = time_g
 
         def finish(t, nh):
-            group, i = group_of(t)
-            if "o" not in group:
-                group["o"] = grp.tile([P, GROUP, N + 1], F32, name="o_grp")
+            if nh == 0:
+                tiles[("o", t)] = opool.tile([P, N + 1], F32, name="o")
             nc.vector.scalar_tensor_tensor(
-                out=group["o"][:, i, 1 + nh * BANK : 1 + (nh + 1) * BANK], in0=tiles[("h", t)][nh][:],
-                scalar=group["a"][:, i : i + 1], in1=bias_s[:, nh * BANK : (nh + 1) * BANK],
+                out=tiles[("o", t)][:, 1 + nh * BANK : 1 + (nh + 1) * BANK], in0=tiles[("h", t, nh)][:],
+                scalar=tiles[("va", t)][:, 3:4], in1=bias_s[:, nh * BANK : (nh + 1) * BANK],
                 op0=ALU.mult, op1=ALU.add,
             )
 
         def store(t):
-            group, i = group_of(t)
-            if i == GROUP - 1:
-                nc.vector.tensor_copy(out=group["o"][:, :, 0], in_=group["time"][:])
-                nc.sync.dma_start(out=out_rows[:, t + 1 - GROUP : t + 1, :], in_=group["o"][:])
+            nc.vector.tensor_copy(out=tiles[("o", t)][:, 0:1], in_=tiles[("time", t)][:])
+            nc.sync.dma_start(out=out_rows[:, t, :], in_=tiles[("o", t)][:])
 
         def live(t):
             return 0 <= t < TILES
 
         def period(j):
+            if live(j + AHEAD_NORM):
+                norm_of_sp(j + AHEAD_NORM)
             if live(j + AHEAD_MATMUL):
                 quantise(j + AHEAD_MATMUL)
+                multiply(j + AHEAD_MATMUL, 0)
             if live(j - 2):
                 time_square_inner(j - 2)
                 finish(j - 2, 0)
+            if live(j + AHEAD_MATMUL):
+                multiply(j + AHEAD_MATMUL, 1)
             if live(j + AHEAD_LOG_MAP):
                 row_scale(j + AHEAD_LOG_MAP)
-            if live(j - 1):
-                bias_dot_sum(j - 1)
             if live(j - 2):
                 time_square(j - 2)
                 finish(j - 2, 1)
-            if live(j + AHEAD_MATMUL):
-                multiply(j + AHEAD_MATMUL)
             if live(j):
                 norm_of_h(j)
                 dot_with_bias(j, 0)
@@ -394,37 +347,26 @@ def tile_hyperboliclinearhyperboloid_kernel(tc, x, weight, bias, out):
                 dot_with_bias(j, 1)
             if live(j - 1):
                 row_factor_sum(j - 1)
-            if live(j + AHEAD_NORM):
-                norm_of_sp(j + AHEAD_NORM)
+            if live(j + AHEAD_REGROUP):
+                regroup(j + AHEAD_REGROUP)
             if live(j + AHEAD_LOG_MAP):
                 log_map(j + AHEAD_LOG_MAP)
             if live(j - 1):
                 row_factor(j - 1)
-            if live(j + AHEAD_REGROUP):
-                regroup(j + AHEAD_REGROUP)
             if live(j - 2):
                 store(j - 2)
 
-        def weight_half(nh):
-            for g in range(PASSES):
-                w_transposes(nh, g)
-            for g in range(PASSES):
-                w_regroup(nh, g)
-            for g in range(PASSES):
-                w_quantise(nh, g)
-
-        bias_spread()
-        bias_root()
-        norm_of_sp(0)
-        norm_of_sp(1)
-        distances()
-        row_scale(0)
-        log_map(0)
-        weight_half(0)
+        period(-4)
+        period(-3)
+        bias_norm()
+        weight_chunk(0)
+        weight_chunk(1)
+        period(-2)
         bias_factors()
-        weight_half(1)
-        for j in range(-2, 1):
-            period(j)
+        weight_chunk(2)
+        weight_chunk(3)
+        period(-1)
+        period(0)
         bias_scaled()
         for j in range(1, TILES + 2):
             period(j)

@@ -42,7 +42,6 @@ def tile_hyperboliclinearhyperboloid_kernel(tc, x, weight, bias, out):
         small = stack.enter_context(tc.tile_pool(name="small", bufs=8))
         psum_t = stack.enter_context(tc.psum_pool(name="psum_t", bufs=1))
         psum_h = stack.enter_context(tc.psum_pool(name="psum_h", bufs=7))
-        stack.enter_context(tc.manual_schedule())
 
         x_rows = x.rearrange("(p t) c -> p t c", t=TILES)
         out_rows = out.rearrange("(p t) c -> p t c", t=TILES)

@@ -42,6 +42,7 @@ def tile_hyperboliclinearhyperboloid_kernel(tc, x, weight, bias, out):
         small = stack.enter_context(tc.tile_pool(name="small", bufs=8))
         psum_t = stack.enter_context(tc.psum_pool(name="psum_t", bufs=1))
         psum_h = stack.enter_context(tc.psum_pool(name="psum_h", bufs=7))
+        stack.enter_context(tc.manual_schedule())
 
         x_rows = x.rearrange("(p t) c -> p t c", t=TILES)
         out_rows = out.rearrange("(p t) c -> p t c", t=TILES)
@@ -226,13 +227,16 @@ def tile_hyperboliclinearhyperboloid_kernel(tc, x, weight, bias, out):
                 )
             tiles[("h", t, nh)] = h
 
-        def norm_of_h(t):
-            hh2 = small.tile([P, BANKS], F32, name="hh2")
-            for nh in range(BANKS):
-                junk_s = junk.tile([P, BANK], F32, name="junk_s")
-                nc.scalar.activation(
-                    out=junk_s[:], in_=tiles[("h", t, nh)][:], func=ACT.Square, accum_out=hh2[:, nh : nh + 1]
-                )
+        def norm_of_h(t, nh):
+            if nh == 0:
+                tiles[("hh2", t)] = small.tile([P, BANKS], F32, name="hh2")
+            junk_s = junk.tile([P, BANK], F32, name="junk_s")
+            nc.scalar.activation(
+                out=junk_s[:], in_=tiles[("h", t, nh)][:], func=ACT.Square, accum_out=tiles[("hh2", t)][:, nh : nh + 1]
+            )
+
+        def radius(t):
+            hh2 = tiles[("hh2", t)]
             hg = small.tile([P, 3], F32, name="hg")
             nc.gpsimd.tensor_scalar(
                 out=hg[:, 0:1], in0=hh2[:, 0:1], scalar1=hh2[:, 1:2], scalar2=1e-30, op0=ALU.add, op1=ALU.max
@@ -264,44 +268,40 @@ def tile_hyperboliclinearhyperboloid_kernel(tc, x, weight, bias, out):
         def row_factor_parts(t):
             ex = tiles[("ex", t)]
             hb = tiles[("hb", t)]
-            va = small.tile([P, 7], F32, name="va")
-            nc.vector.scalar_tensor_tensor(
-                out=va[:, 0:1], in0=hb[:, 0:1], scalar=hb[:, 1:2], in1=ex[:, 2:3], op0=ALU.add, op1=ALU.mult
-            )
-            nc.vector.scalar_tensor_tensor(
-                out=va[:, 1:2], in0=ex[:, 0:1], scalar=ex[:, 1:2], in1=tiles[("hg", t)][:, 1:2],
-                op0=ALU.subtract, op1=ALU.mult,
-            )
-            nc.vector.tensor_scalar(
-                out=va[:, 4:5], in0=hb[:, 0:1], scalar1=hb[:, 1:2], scalar2=4.0, op0=ALU.add, op1=ALU.mult
-            )
-            tiles[("va", t)] = va
+            r_inv = tiles[("hg", t)][:, 1:2]
+            sx = small.tile([P, 6], F32, name="sx")
+            nc.scalar.activation(out=sx[:, 0:1], in_=ex[:, 1:2], func=ACT.Identity, scale=-1.0, bias=ex[:, 0:1])
+            nc.scalar.activation(out=sx[:, 1:2], in_=ex[:, 2:3], func=ACT.Copy, scale=r_inv)
+            nc.scalar.activation(out=sx[:, 2:3], in_=hb[:, 0:1], func=ACT.Identity, scale=1.0, bias=hb[:, 1:2])
+            tiles[("sx", t)] = sx
 
-        def row_factor_sum(t):
-            va = tiles[("va", t)]
-            nc.vector.tensor_scalar(
-                out=va[:, 2:3], in0=va[:, 0:1], scalar1=tiles[("hg", t)][:, 1:2], scalar2=cosh_half,
-                op0=ALU.mult, op1=ALU.add,
-            )
+        def row_factor_products(t):
+            sx = tiles[("sx", t)]
+            nc.scalar.activation(out=sx[:, 3:4], in_=sx[:, 0:1], func=ACT.Copy, scale=tiles[("hg", t)][:, 1:2])
+            nc.scalar.activation(out=sx[:, 4:5], in_=sx[:, 2:3], func=ACT.Identity, scale=sx[:, 1:2], bias=cosh_half)
 
         def row_factor(t):
-            va = tiles[("va", t)]
-            nc.vector.tensor_tensor(out=va[:, 3:4], in0=va[:, 2:3], in1=va[:, 1:2], op=ALU.mult)
+            sx = tiles[("sx", t)]
+            nc.scalar.activation(out=sx[:, 5:6], in_=sx[:, 4:5], func=ACT.Copy, scale=sx[:, 3:4])
+
+        def time_square_first(t):
+            sy = small.tile([P, 3], F32, name="sy")
+            nc.scalar.activation(out=sy[:, 0:1], in_=tiles[("hg", t)][:, 0:1], func=ACT.Copy, scale=tiles[("sx", t)][:, 5:6])
+            tiles[("sy", t)] = sy
 
         def time_square_inner(t):
-            va = tiles[("va", t)]
-            nc.vector.tensor_scalar(
-                out=va[:, 5:6], in0=tiles[("hg", t)][:, 0:1], scalar1=va[:, 3:4], scalar2=va[:, 4:5],
-                op0=ALU.mult, op1=ALU.add,
+            sy = tiles[("sy", t)]
+            nc.scalar.activation(
+                out=sy[:, 1:2], in_=tiles[("sx", t)][:, 2:3], func=ACT.Identity, scale=4.0, bias=sy[:, 0:1]
             )
 
         def time_square(t):
-            va = tiles[("va", t)]
-            nc.vector.tensor_scalar(
-                out=va[:, 6:7], in0=va[:, 5:6], scalar1=va[:, 3:4], scalar2=one_plus, op0=ALU.mult, op1=ALU.add
+            sy = tiles[("sy", t)]
+            nc.scalar.activation(
+                out=sy[:, 2:3], in_=sy[:, 1:2], func=ACT.Identity, scale=tiles[("sx", t)][:, 5:6], bias=one_plus
             )
             time_g = small.tile([P, 1], F32, name="time_g")
-            nc.gpsimd.tensor_tensor(out=time_g[:], in0=va[:, 6:7], in1=half[:], op=ALU.pow)
+            nc.gpsimd.tensor_tensor(out=time_g[:], in0=sy[:, 2:3], in1=half[:], op=ALU.pow)
             tiles[("time", t)] = time_g
 
         def finish(t, nh):
@@ -309,7 +309,7 @@ def tile_hyperboliclinearhyperboloid_kernel(tc, x, weight, bias, out):
                 tiles[("o", t)] = opool.tile([P, N + 1], F32, name="o")
             nc.vector.scalar_tensor_tensor(
                 out=tiles[("o", t)][:, 1 + nh * BANK : 1 + (nh + 1) * BANK], in0=tiles[("h", t, nh)][:],
-                scalar=tiles[("va", t)][:, 3:4], in1=bias_s[:, nh * BANK : (nh + 1) * BANK],
+                scalar=tiles[("sx", t)][:, 5:6], in1=bias_s[:, nh * BANK : (nh + 1) * BANK],
                 op0=ALU.mult, op1=ALU.add,
             )
 
@@ -323,37 +323,44 @@ def tile_hyperboliclinearhyperboloid_kernel(tc, x, weight, bias, out):
         def period(j):
             if live(j + AHEAD_NORM):
                 norm_of_sp(j + AHEAD_NORM)
+            if live(j - 2):
+                row_factor(j - 2)
             if live(j + AHEAD_MATMUL):
                 quantise(j + AHEAD_MATMUL)
                 multiply(j + AHEAD_MATMUL, 0)
             if live(j - 2):
-                time_square_inner(j - 2)
                 finish(j - 2, 0)
             if live(j + AHEAD_MATMUL):
                 multiply(j + AHEAD_MATMUL, 1)
             if live(j + AHEAD_LOG_MAP):
                 row_scale(j + AHEAD_LOG_MAP)
             if live(j - 2):
-                time_square(j - 2)
                 finish(j - 2, 1)
             if live(j):
-                norm_of_h(j)
+                norm_of_h(j, 0)
                 dot_with_bias(j, 0)
             if live(j - 1):
                 exponentials(j - 1)
-                row_factor_parts(j - 1)
+            if live(j - 2):
+                time_square_first(j - 2)
             if live(j):
+                norm_of_h(j, 1)
+                radius(j)
                 dot_with_bias(j, 1)
             if live(j - 1):
-                row_factor_sum(j - 1)
+                row_factor_parts(j - 1)
+            if live(j - 2):
+                time_square_inner(j - 2)
             if live(j + AHEAD_REGROUP):
                 regroup(j + AHEAD_REGROUP)
+            if live(j - 1):
+                row_factor_products(j - 1)
+            if live(j - 2):
+                time_square(j - 2)
             if live(j + AHEAD_LOG_MAP):
                 log_map(j + AHEAD_LOG_MAP)
-            if live(j - 1):
-                row_factor(j - 1)
-            if live(j - 2):
-                store(j - 2)
+            if live(j - 3):
+                store(j - 3)
 
         period(-4)
         period(-3)
@@ -367,5 +374,5 @@ def tile_hyperboliclinearhyperboloid_kernel(tc, x, weight, bias, out):
         period(-1)
         period(0)
         bias_scaled()
-        for j in range(1, TILES + 2):
+        for j in range(1, TILES + 3):
             period(j)

from contextlib import ExitStack

import concourse.mybir as mybir
from concourse.masks import make_identity

FP8X4 = mybir.dt.float8_e4m3fn_x4
BF16 = mybir.dt.bfloat16
F32 = mybir.dt.float32
U32 = mybir.dt.uint32
U8 = mybir.dt.uint8
ALU = mybir.AluOpType
ACT = mybir.ActivationFunctionType

P = 128
ROWS = 2048
K = 1024
N = 1024
TILES = ROWS // P
K_PASS = 512
PASSES = K // K_PASS
BANK = 512
BANKS = N // BANK
W_CHUNK = 256
W_CHUNKS = N // W_CHUNK
X_SLOT = 1040
AHEAD_NORM = 4
AHEAD_LOG_MAP = 3
AHEAD_REGROUP = 2
AHEAD_MATMUL = 1

FLOPS = 2 * ROWS * K * N


def tile_hyperboliclinearhyperboloid_kernel(tc, x, weight, bias, out):
    nc = tc.nc
    with ExitStack() as stack:
        keep = stack.enter_context(tc.tile_pool(name="keep", bufs=1))
        wstage = stack.enter_context(tc.tile_pool(name="wstage", bufs=4))
        upool = stack.enter_context(tc.tile_pool(name="upool", bufs=4))
        opool = stack.enter_context(tc.tile_pool(name="opool", bufs=4))
        junk = stack.enter_context(tc.tile_pool(name="junk", bufs=3))
        small = stack.enter_context(tc.tile_pool(name="small", bufs=8))
        psum_t = stack.enter_context(tc.psum_pool(name="psum_t", bufs=1))
        psum_h = stack.enter_context(tc.psum_pool(name="psum_h", bufs=7))
        stack.enter_context(tc.manual_schedule())

        x_rows = x.rearrange("(p t) c -> p t c", t=TILES)
        out_rows = out.rearrange("(p t) c -> p t c", t=TILES)
        w_rows = weight.rearrange("(c b p) k -> p c b k", b=W_CHUNK // P, p=P)

        x_head = keep.tile([P, TILES, 16], BF16)
        bias_bc = keep.tile([P, N], BF16)
        x_sb = keep.tile([P, TILES, X_SLOT], BF16)
        w_sb = keep.tile([P, W_CHUNKS, W_CHUNK // P, K], BF16)

        def load_x(t0, t1):
            nc.sync.dma_start(out=x_sb[:, t0:t1, 1 : K + 2], in_=x_rows[:, t0:t1, :])

        def load_w(c):
            nc.sync.dma_start(out=w_sb[:, c, :, :], in_=w_rows[:, c, :, :])

        nc.sync.dma_start(out=x_head[:], in_=x_rows[:, :, 0:16])
        load_x(0, 2)
        nc.sync.dma_start(out=bias_bc[:], in_=bias.rearrange("a b -> (a b)").partition_broadcast(P))
        load_w(0)
        load_w(1)
        load_x(2, 4)
        load_w(2)
        load_w(3)
        load_x(4, 6)
        load_x(6, 8)
        load_x(8, 12)
        load_x(12, 16)

        ident_f = keep.tile([P, P], F32)
        make_identity(nc, ident_f[:])
        half = keep.tile([P, 1], F32)
        nc.vector.memset(half[:], 0.5)
        minus_half = keep.tile([P, 1], F32)
        nc.vector.memset(minus_half[:], -0.5)
        warm = keep.tile([P, 1], F32)
        nc.scalar.activation(out=warm[:], in_=half[:], func=ACT.Sqrt)

        theta0 = keep.tile([P, TILES], F32)
        nc.vector.tensor_scalar(out=theta0[:], in0=x_head[:, :, 0], scalar1=1.0 + 1e-7, scalar2=None, op0=ALU.max)
        theta0_m1 = keep.tile([P, TILES], F32)
        nc.vector.tensor_scalar(out=theta0_m1[:], in0=theta0[:], scalar1=-1.0, scalar2=None, op0=ALU.add)
        theta0_sq = keep.tile([P, TILES], F32)
        nc.vector.scalar_tensor_tensor(
            out=theta0_sq[:], in0=theta0[:], scalar=1.0, in1=theta0_m1[:], op0=ALU.add, op1=ALU.mult
        )
        theta0_rt = keep.tile([P, TILES], F32)
        nc.scalar.activation(out=theta0_rt[:], in_=theta0_sq[:], func=ACT.Sqrt)
        theta0_sum = keep.tile([P, TILES], F32)
        nc.vector.tensor_tensor(out=theta0_sum[:], in0=theta0[:], in1=theta0_rt[:], op=ALU.add)
        dist = keep.tile([P, TILES], F32)
        nc.scalar.activation(out=dist[:], in_=theta0_sum[:], func=ACT.Ln)

        bb = keep.tile([P, 1], F32)
        t_g = keep.tile([P, 3], F32)
        t_b = t_g[:, 2:3]
        t_e = keep.tile([P, 2], F32)
        t_v = keep.tile([P, 6], F32)
        t_inv = t_v[:, 0:1]
        cosh_half = t_v[:, 1:2]
        sinc2 = t_v[:, 2:3]
        sinc_quarter = t_v[:, 3:4]
        one_plus = t_v[:, 5:6]
        bias_s = keep.tile([P, N], F32)

        def bias_norm():
            junk_b = junk.tile([P, N], F32, tag="junk_a")
            nc.vector.scalar_tensor_tensor(
                out=junk_b[:], in0=bias_bc[:], scalar=1.0, in1=bias_bc[:], op0=ALU.mult, op1=ALU.mult, accum_out=bb[:]
            )
            nc.gpsimd.tensor_scalar(out=t_g[:, 0:1], in0=bb[:], scalar1=1e-15, scalar2=None, op0=ALU.max)
            nc.gpsimd.tensor_tensor(out=t_g[:, 1:2], in0=t_g[:, 0:1], in1=half[:], op=ALU.pow)
            nc.gpsimd.tensor_scalar(out=t_b, in0=t_g[:, 1:2], scalar1=1e-15, scalar2=15.0, op0=ALU.max, op1=ALU.min)

        def bias_factors():
            nc.scalar.activation(out=t_e[:, 0:1], in_=t_b, func=ACT.Exp)
            nc.scalar.activation(out=t_e[:, 1:2], in_=t_b, func=ACT.Exp, scale=-1.0)
            nc.vector.reciprocal(out=t_inv, in_=t_b)
            nc.vector.tensor_scalar(
                out=cosh_half, in0=t_e[:, 0:1], scalar1=t_e[:, 1:2], scalar2=0.25, op0=ALU.add, op1=ALU.mult
            )
            nc.vector.scalar_tensor_tensor(
                out=sinc2, in0=t_e[:, 0:1], scalar=t_e[:, 1:2], in1=t_inv, op0=ALU.subtract, op1=ALU.mult
            )
            nc.vector.tensor_scalar(out=sinc_quarter, in0=sinc2, scalar1=0.25, scalar2=None, op0=ALU.mult)
            nc.vector.scalar_tensor_tensor(
                out=t_v[:, 4:5], in0=sinc2, scalar=sinc2, in1=bb[:], op0=ALU.mult, op1=ALU.mult
            )
            nc.vector.tensor_scalar(out=one_plus, in0=t_v[:, 4:5], scalar1=0.25, scalar2=1.0, op0=ALU.mult, op1=ALU.add)

        def bias_scaled():
            nc.vector.tensor_scalar(
                out=bias_s[:], in0=bias_bc[:], scalar1=sinc2, scalar2=0.5, op0=ALU.mult, op1=ALU.mult
            )

        w_codes = keep.tile([P, PASSES, N], U32, align_bytes=64)
        w_scales = keep.tile([P, PASSES, N], U8, align_bytes=64)
        w_words = w_sb[:].bitcast(F32)

        def weight_chunk(c):
            grouped = []
            for g in range(PASSES):
                wt = psum_h.tile([P, 2, W_CHUNK], F32, tag="h", name="wt")
                for u in range(2):
                    for b in range(W_CHUNK // P):
                        nc.tensor.transpose(
                            wt[:, u, b * P : (b + 1) * P],
                            w_words[:, c, b, 256 * g + P * u : 256 * g + P * (u + 1)],
                            ident_f[:],
                        )
                w_grouped = wstage.tile([P, W_CHUNK, 4], BF16, align_bytes=64, name="w_grouped")
                if g == 0:
                    nc.vector.tensor_copy(out=w_grouped[:].bitcast(F32), in_=wt[:].rearrange("p u n -> p n u"))
                else:
                    nc.scalar.copy(out=w_grouped[:].bitcast(F32), in_=wt[:].rearrange("p u n -> p n u"))
                grouped.append(w_grouped)
            n_cols = slice(c * W_CHUNK, (c + 1) * W_CHUNK)
            for g in reversed(range(PASSES)):
                nc.vector.quantize_mx(
                    out=w_codes[:, g, n_cols].bitcast(FP8X4),
                    scales=w_scales[:, g, n_cols],
                    in_=grouped[g][:].rearrange("p n j -> p (n j)"),
                )

        tiles = {}

        def sp(t):
            return x_sb[:, t, 2 : K + 2]

        def norm_of_sp(t):
            junk_a = junk.tile([P, K], F32, tag="junk_a", name="junk_a")
            ss = small.tile([P, 1], F32, name="ss")
            nc.scalar.activation(out=junk_a[:], in_=sp(t), func=ACT.Square, accum_out=ss[:])
            rn = small.tile([P, 1], F32, name="rn")
            nc.gpsimd.tensor_tensor(out=rn[:], in0=ss[:], in1=minus_half[:], op=ALU.pow)
            tiles[("rn", t)] = rn

        def row_scale(t):
            s_row = small.tile([P, 1], F32, name="s_row")
            nc.vector.tensor_scalar(
                out=s_row[:], in0=tiles[("rn", t)][:], scalar1=1e15, scalar2=dist[:, t : t + 1], op0=ALU.min, op1=ALU.mult
            )
            tiles[("s", t)] = s_row

        def log_map(t):
            u_bf = upool.tile([P, K], BF16, name="u_bf")
            nc.vector.tensor_scalar(out=u_bf[:], in0=sp(t), scalar1=tiles[("s", t)][:], scalar2=None, op0=ALU.mult)
            ut = psum_t.tile([P, PASSES, 2, P], F32, name="ut")
            u_words = u_bf[:].bitcast(F32)
            for g in range(PASSES):
                for u in range(2):
                    nc.tensor.transpose(ut[:, g, u, :], u_words[:, 256 * g + P * u : 256 * g + P * (u + 1)], ident_f[:])
            tiles[("ut", t)] = ut

        def regroup(t):
            u_grouped = upool.tile([P, PASSES, P, 4], BF16, align_bytes=64, name="u_grouped")
            nc.scalar.copy(out=u_grouped[:].bitcast(F32), in_=tiles[("ut", t)][:].rearrange("p g u m -> p g m u"))
            tiles[("ug", t)] = u_grouped

        def quantise(t):
            u_codes = upool.tile([P, PASSES * P], U32, align_bytes=64, name="u_codes")
            u_scales = upool.tile([P, PASSES * P], U8, align_bytes=64, name="u_scales")
            nc.vector.quantize_mx(
                out=u_codes[:].bitcast(FP8X4),
                scales=u_scales[:],
                in_=tiles[("ug", t)][:].rearrange("p g m j -> p (g m j)"),
            )
            tiles[("uq", t)] = (u_codes, u_scales)

        def multiply(t, nh):
            u_codes, u_scales = tiles[("uq", t)]
            h = psum_h.tile([P, BANK], F32, tag="h", name="h")
            for g in range(PASSES):
                nc.tensor.matmul_mx(
                    out=h[:],
                    lhsT=u_codes[:, g * P : (g + 1) * P].bitcast(FP8X4),
                    lhsT_scale=u_scales[:, g * P : (g + 1) * P],
                    rhs=w_codes[:, g, nh * BANK : (nh + 1) * BANK].bitcast(FP8X4),
                    rhs_scale=w_scales[:, g, nh * BANK : (nh + 1) * BANK],
                    start=(g == 0),
                    stop=(g == PASSES - 1),
                )
            tiles[("h", t, nh)] = h

        def norm_of_h(t, nh):
            if nh == 0:
                tiles[("hh2", t)] = small.tile([P, BANKS], F32, name="hh2")
            junk_s = junk.tile([P, BANK], F32, name="junk_s")
            nc.scalar.activation(
                out=junk_s[:], in_=tiles[("h", t, nh)][:], func=ACT.Square, accum_out=tiles[("hh2", t)][:, nh : nh + 1]
            )

        def radius(t):
            hh2 = tiles[("hh2", t)]
            hg = small.tile([P, 3], F32, name="hg")
            nc.gpsimd.tensor_scalar(
                out=hg[:, 0:1], in0=hh2[:, 0:1], scalar1=hh2[:, 1:2], scalar2=1e-30, op0=ALU.add, op1=ALU.max
            )
            nc.gpsimd.tensor_tensor(out=hg[:, 1:2], in0=hg[:, 0:1], in1=minus_half[:], op=ALU.pow)
            nc.gpsimd.tensor_scalar(
                out=hg[:, 2:3], in0=hg[:, 0:1], scalar1=hg[:, 1:2], scalar2=15.0, op0=ALU.mult, op1=ALU.min
            )
            tiles[("hg", t)] = hg

        def dot_with_bias(t, nh):
            if nh == 0:
                tiles[("hb", t)] = small.tile([P, BANKS], F32, name="hb")
            junk_v = junk.tile([P, BANK], F32, name="junk_v")
            nc.vector.scalar_tensor_tensor(
                out=junk_v[:], in0=tiles[("h", t, nh)][:], scalar=sinc_quarter,
                in1=bias_bc[:, nh * BANK : (nh + 1) * BANK],
                op0=ALU.mult, op1=ALU.mult, accum_out=tiles[("hb", t)][:, nh : nh + 1],
            )

        def exponentials(t):
            theta = tiles[("hg", t)][:, 2:3]
            ex = small.tile([P, 3], F32, name="ex")
            nc.scalar.activation(out=ex[:, 0:1], in_=theta, func=ACT.Exp)
            nc.scalar.activation(out=ex[:, 1:2], in_=theta, func=ACT.Exp, scale=-1.0)
            nc.scalar.activation(out=ex[:, 2:3], in_=theta, func=ACT.Tanh, scale=0.5)
            tiles[("ex", t)] = ex

        def row_factor_parts(t):
            ex = tiles[("ex", t)]
            hb = tiles[("hb", t)]
            r_inv = tiles[("hg", t)][:, 1:2]
            sx = small.tile([P, 6], F32, name="sx")
            nc.scalar.activation(out=sx[:, 0:1], in_=ex[:, 1:2], func=ACT.Identity, scale=-1.0, bias=ex[:, 0:1])
            nc.scalar.activation(out=sx[:, 1:2], in_=ex[:, 2:3], func=ACT.Copy, scale=r_inv)
            nc.scalar.activation(out=sx[:, 2:3], in_=hb[:, 0:1], func=ACT.Identity, scale=1.0, bias=hb[:, 1:2])
            tiles[("sx", t)] = sx

        def row_factor_products(t):
            sx = tiles[("sx", t)]
            nc.scalar.activation(out=sx[:, 3:4], in_=sx[:, 0:1], func=ACT.Copy, scale=tiles[("hg", t)][:, 1:2])
            nc.scalar.activation(out=sx[:, 4:5], in_=sx[:, 2:3], func=ACT.Identity, scale=sx[:, 1:2], bias=cosh_half)

        def row_factor(t):
            sx = tiles[("sx", t)]
            nc.scalar.activation(out=sx[:, 5:6], in_=sx[:, 4:5], func=ACT.Copy, scale=sx[:, 3:4])

        def time_square_first(t):
            sy = small.tile([P, 3], F32, name="sy")
            nc.scalar.activation(out=sy[:, 0:1], in_=tiles[("hg", t)][:, 0:1], func=ACT.Copy, scale=tiles[("sx", t)][:, 5:6])
            tiles[("sy", t)] = sy

        def time_square_inner(t):
            sy = tiles[("sy", t)]
            nc.scalar.activation(
                out=sy[:, 1:2], in_=tiles[("sx", t)][:, 2:3], func=ACT.Identity, scale=4.0, bias=sy[:, 0:1]
            )

        def time_square(t):
            sy = tiles[("sy", t)]
            nc.scalar.activation(
                out=sy[:, 2:3], in_=sy[:, 1:2], func=ACT.Identity, scale=tiles[("sx", t)][:, 5:6], bias=one_plus
            )
            time_g = small.tile([P, 1], F32, name="time_g")
            nc.gpsimd.tensor_tensor(out=time_g[:], in0=sy[:, 2:3], in1=half[:], op=ALU.pow)
            tiles[("time", t)] = time_g

        def finish(t, nh):
            if nh == 0:
                tiles[("o", t)] = opool.tile([P, N + 1], F32, name="o")
            nc.vector.scalar_tensor_tensor(
                out=tiles[("o", t)][:, 1 + nh * BANK : 1 + (nh + 1) * BANK], in0=tiles[("h", t, nh)][:],
                scalar=tiles[("sx", t)][:, 5:6], in1=bias_s[:, nh * BANK : (nh + 1) * BANK],
                op0=ALU.mult, op1=ALU.add,
            )

        def store(t):
            nc.vector.tensor_copy(out=tiles[("o", t)][:, 0:1], in_=tiles[("time", t)][:])
            nc.sync.dma_start(out=out_rows[:, t, :], in_=tiles[("o", t)][:])

        def live(t):
            return 0 <= t < TILES

        def period(j):
            if live(j + AHEAD_NORM):
                norm_of_sp(j + AHEAD_NORM)
            if live(j - 2):
                row_factor(j - 2)
            if live(j + AHEAD_MATMUL):
                quantise(j + AHEAD_MATMUL)
                multiply(j + AHEAD_MATMUL, 0)
            if live(j - 2):
                finish(j - 2, 0)
            if live(j + AHEAD_MATMUL):
                multiply(j + AHEAD_MATMUL, 1)
            if live(j + AHEAD_LOG_MAP):
                row_scale(j + AHEAD_LOG_MAP)
            if live(j - 2):
                finish(j - 2, 1)
            if live(j):
                norm_of_h(j, 0)
                dot_with_bias(j, 0)
            if live(j - 1):
                exponentials(j - 1)
            if live(j - 2):
                time_square_first(j - 2)
            if live(j):
                norm_of_h(j, 1)
                radius(j)
                dot_with_bias(j, 1)
            if live(j - 1):
                row_factor_parts(j - 1)
            if live(j - 2):
                time_square_inner(j - 2)
            if live(j + AHEAD_REGROUP):
                regroup(j + AHEAD_REGROUP)
            if live(j - 1):
                row_factor_products(j - 1)
            if live(j - 2):
                time_square(j - 2)
            if live(j + AHEAD_LOG_MAP):
                log_map(j + AHEAD_LOG_MAP)
            if live(j - 3):
                store(j - 3)

        period(-4)
        period(-3)
        bias_norm()
        weight_chunk(0)
        weight_chunk(1)
        period(-2)
        bias_factors()
        weight_chunk(2)
        weight_chunk(3)
        period(-1)
        period(0)
        bias_scaled()
        for j in range(1, TILES + 3):
            period(j)
